import numpy as np
import ml_dtypes


def mxq(x, axis, fmt="e4m3"):
    dtype, down = {"e4m3": (ml_dtypes.float8_e4m3fn, 7), "e5m2": (ml_dtypes.float8_e5m2, 14)}[fmt]
    v = np.moveaxis(np.asarray(x, np.float32).astype(ml_dtypes.bfloat16).astype(np.float64), axis, -1)
    blocks = v.reshape(v.shape[:-1] + (-1, 32))
    amax = np.abs(blocks).max(-1, keepdims=True)
    byte = np.maximum(np.where(amax > 0, np.frexp(amax)[1] - 1 + 127, 0) - down, 1)
    scale = np.exp2(byte - 127.0)
    codes = (blocks / scale).astype(np.float32).astype(dtype).astype(np.float64)
    return np.moveaxis((codes * scale).reshape(v.shape), -1, axis)


WIDE = False


def mx_kscale(k):
    if not WIDE:
        return np.ones(k)
    levels = np.array([10, -10, 5, -5, 0])
    a = np.random.permutation(np.resize(levels, k // 512 * 4)).reshape(k // 512, 4)
    idx = np.arange(k)
    return np.exp2(a[idx // 512, idx % 128 // 32])


BF16 = ml_dtypes.bfloat16


def bf(x):
    return np.asarray(x, np.float32).astype(BF16)


def f64(x):
    return np.asarray(x).astype(np.float64)


U, V, CI, CO = 512, 512, 512, 128
N = U + V
AVG_DEG = 32.0
LEAKY_SLOPE = 0.01


def setup_inputs():
    s = mx_kscale(CI)
    mask = np.random.random_sample((N, N)) < AVG_DEG / N
    adj = mask * (0.5 + np.random.random_sample((N, N)))
    return {"x": bf(np.random.standard_normal((N, CI)) * s),
            "adj": bf(adj),
            "weightr": bf(np.random.standard_normal((CI, CO)) * 3.0 / np.sqrt(CI) / s[:, None]),
            "weightd": bf(np.random.standard_normal((CI, CO)) * 3.0 / np.sqrt(CI) / s[:, None]),
            "bias": bf(np.random.standard_normal(CO) * 0.1)}


def reference(x, adj, weightr, weightd, bias):
    A = f64(adj) + np.eye(N)
    deg = A.sum(axis=1)
    dinv = np.where(deg > 0, 1.0 / np.sqrt(np.where(deg > 0, deg, 1.0)), 0.0)
    A = A * dinv[:, None] * dinv[None, :]
    xq = mxq(f64(x), 1, "e4m3")
    R = xq[:U] @ mxq(f64(weightr), 0, "e4m3")
    D = xq[U:] @ mxq(f64(weightd), 0, "e4m3")
    h = np.concatenate([R, D], axis=0)
    out = (mxq(A, 1, "e4m3") @ mxq(h, 0, "e4m3")) + f64(bias)
    return np.where(out >= 0, out, LEAKY_SLOPE * out)

@@ -1,0 +1,220 @@
+from contextlib import ExitStack
+
+import concourse.mybir as mybir
+from concourse.masks import make_identity
+
+FP8X4 = mybir.dt.float8_e4m3fn_x4
+BF16 = mybir.dt.bfloat16
+F32 = mybir.dt.float32
+U32 = mybir.dt.uint32
+U8 = mybir.dt.uint8
+ALU = mybir.AluOpType
+ACT = mybir.ActivationFunctionType
+
+P = 128
+PACK = 4
+NODES = 1024
+FEATS = 512
+CO = 128
+TILES = NODES // P
+PASSES = NODES // (P * PACK)
+QUANT_TILES = 2
+LEAKY_SLOPE = 0.01
+
+FLOPS = 2 * NODES * FEATS * CO + 2 * NODES * NODES * CO
+
+
+def tile_gcnconv_s_kernel(tc, x, adj, weightr, weightd, bias, out):
+    nc = tc.nc
+    with ExitStack() as ctx:
+        keep = ctx.enter_context(tc.tile_pool(name="keep", bufs=1))
+        scrap_pool = ctx.enter_context(tc.tile_pool(name="scrap", bufs=2))
+        result_pool = ctx.enter_context(tc.tile_pool(name="result", bufs=2))
+        flip_psum = ctx.enter_context(tc.psum_pool(name="flip", bufs=4))
+        sum_psum = ctx.enter_context(tc.psum_pool(name="sums", bufs=1))
+
+        adj_rows = adj.rearrange("(m p) j -> m p j", p=P)
+        adj_sb = []
+        for m in range(TILES):
+            adj_m = keep.tile([P, NODES], BF16, name="adj%d" % m)
+            nc.sync.dma_start(out=adj_m[:], in_=adj_rows[m])
+            adj_sb.append(adj_m)
+        w_raw = keep.tile([P, 2, PACK, CO], BF16)
+        for w, weight in enumerate((weightr, weightd)):
+            nc.sync.dma_start(
+                out=w_raw[:, w].rearrange("p (u e) c -> p u (e c)", e=2),
+                in_=weight.rearrange("(u p e) c -> p u (e c)", u=2, e=2),
+            )
+        x_sb = keep.tile([P, TILES, FEATS], BF16)
+        x_rows = x.rearrange("(n p) k -> p n k", p=P)
+        for half in range(2):
+            tiles = slice(half * TILES // 2, (half + 1) * TILES // 2)
+            nc.sync.dma_start(out=x_sb[:, tiles, :], in_=x_rows[:, tiles, :])
+        bias_all = keep.tile([P, CO], BF16)
+        nc.sync.dma_start(out=bias_all[:], in_=bias.partition_broadcast(P))
+
+        ident = keep.tile([P, P], F32)
+        make_identity(nc, ident[:])
+
+        one = keep.tile([P, 1], F32)
+        nc.vector.memset(one[:], 1.0)
+        warm = keep.tile([P, 1], F32)
+        nc.scalar.activation(out=warm[:], in_=one[:], func=ACT.Abs_reciprocal_sqrt)
+
+        deg = keep.tile([P, TILES], F32)
+        dinv = [keep.tile([P, PACK], F32, name="dinv%d" % g) for g in range(PASSES)]
+        scaled = []
+        loop_scaled = []
+        for m in range(TILES):
+            g, t = divmod(m, PACK)
+            dinv_m = dinv[g][:, t : t + 1]
+            scrap = scrap_pool.tile([P, NODES], BF16)
+            nc.vector.tensor_scalar(
+                out=scrap[:],
+                in0=adj_sb[m][:],
+                scalar1=1.0,
+                scalar2=1.0,
+                op0=ALU.mult,
+                op1=ALU.add,
+                accum_out=deg[:, m : m + 1],
+            )
+            nc.scalar.activation(out=dinv_m, in_=deg[:, m : m + 1], func=ACT.Abs_reciprocal_sqrt)
+            scaled_m = keep.tile([P, NODES], F32, name="scaled%d" % m)
+            nc.scalar.activation(out=scaled_m[:], in_=adj_sb[m][:], func=ACT.Copy, scale=dinv_m)
+            scaled.append(scaled_m)
+            loop_m = keep.tile([P, P], F32, name="loop%d" % m)
+            nc.gpsimd.tensor_tensor(
+                out=loop_m[:], in0=adj_sb[m][:, m * P : (m + 1) * P], in1=ident[:], op=ALU.add
+            )
+            loop_scaled_m = keep.tile([P, P], F32, name="loop_scaled%d" % m)
+            nc.gpsimd.tensor_scalar(
+                out=loop_scaled_m[:],
+                in0=loop_m[:],
+                scalar1=dinv_m,
+                scalar2=0.0,
+                op0=ALU.mult,
+                op1=ALU.add,
+            )
+            loop_scaled.append(loop_scaled_m)
+
+        w_grouped = keep.tile([P, 2, CO, PACK], BF16, align_bytes=64)
+        nc.scalar.copy(out=w_grouped[:], in_=w_raw[:].rearrange("p w t c -> p w c t"))
+        w_codes = keep.tile([P, 2, CO], U32, align_bytes=64)
+        w_scales = keep.tile([P, 2, CO], U8, align_bytes=64)
+        nc.vector.quantize_mx(
+            out=w_codes[:].rearrange("p w c -> p (w c)").bitcast(FP8X4),
+            scales=w_scales[:].rearrange("p w c -> p (w c)"),
+            in_=w_grouped[:].rearrange("p w c t -> p (w c t)"),
+        )
+        x_grouped = keep.tile([P, NODES, PACK], BF16, align_bytes=64)
+        x_words = x_grouped[:].bitcast(F32)
+        x_codes = keep.tile([P, NODES], U32, align_bytes=64)
+        x_scales = keep.tile([P, NODES], U8, align_bytes=64)
+        for pair in range(TILES // 2):
+            flipped = flip_psum.tile([P, 2, 2, P], F32, tag="bank")
+            for n2 in range(2):
+                for u in range(2):
+                    nc.tensor.transpose(
+                        flipped[:, n2, u, :],
+                        x_sb[:, 2 * pair + n2, :].bitcast(F32)[:, u * P : (u + 1) * P],
+                        ident[:],
+                    )
+            nc.scalar.copy(
+                out=x_words[:, 2 * pair * P : (2 * pair + 2) * P, :].rearrange(
+                    "p (n r) u -> p n r u", n=2
+                ),
+                in_=flipped[:].rearrange("p n u r -> p n r u"),
+            )
+        for half in range(2):
+            nodes = slice(half * NODES // 2, (half + 1) * NODES // 2)
+            nc.vector.quantize_mx(
+                out=x_codes[:, nodes].bitcast(FP8X4),
+                scales=x_scales[:, nodes],
+                in_=x_grouped[:, nodes, :].rearrange("p r t -> p (r t)"),
+            )
+        h_grouped = keep.tile([P, PASSES, CO, PACK], BF16, align_bytes=64)
+        for g in range(PASSES):
+            h_sum = sum_psum.tile([P, PACK, CO], F32, name="h_sum%d" % g)
+            for t in range(PACK):
+                n = PACK * g + t
+                nc.tensor.matmul_mx(
+                    out=h_sum[:, t, :],
+                    lhsT=x_codes[:, n * P : (n + 1) * P].bitcast(FP8X4),
+                    lhsT_scale=x_scales[:, n * P : (n + 1) * P],
+                    rhs=w_codes[:, g, :].bitcast(FP8X4),
+                    rhs_scale=w_scales[:, g, :],
+                    start=True,
+                    stop=True,
+                )
+            nc.scalar.copy(out=h_grouped[:, g], in_=h_sum[:].rearrange("p t c -> p c t"))
+        h_codes = keep.tile([P, PASSES, CO], U32, align_bytes=64)
+        h_scales = keep.tile([P, PASSES, CO], U8, align_bytes=64)
+        nc.vector.quantize_mx(
+            out=h_codes[:].rearrange("p g c -> p (g c)").bitcast(FP8X4),
+            scales=h_scales[:].rearrange("p g c -> p (g c)"),
+            in_=h_grouped[:].rearrange("p g c t -> p (g c t)"),
+        )
+
+        a_codes = []
+        a_scales = []
+        for g in range(PASSES):
+            a_grouped = keep.tile([P, TILES, P, PACK], BF16, name="a_grouped%d" % g, align_bytes=64)
+            a_codes_g = keep.tile([P, TILES, P], U32, name="a_codes%d" % g, align_bytes=64)
+            a_scales_g = keep.tile([P, TILES, P], U8, name="a_scales%d" % g, align_bytes=64)
+            for m in range(TILES):
+                flipped = flip_psum.tile([P, PACK, P], F32, tag="bank")
+                for t in range(PACK):
+                    block = PACK * g + t
+                    if block == m:
+                        rows = loop_scaled[m][:]
+                    else:
+                        rows = scaled[m][:, block * P : (block + 1) * P]
+                    nc.tensor.transpose(flipped[:, t, :], rows, ident[:])
+                nc.vector.tensor_tensor(
+                    out=a_grouped[:, m],
+                    in0=flipped[:].rearrange("p t i -> p i t"),
+                    in1=dinv[g][:].unsqueeze(1).to_broadcast([P, P, PACK]),
+                    op=ALU.mult,
+                )
+                if m % QUANT_TILES == QUANT_TILES - 1:
+                    tiles = slice(m + 1 - QUANT_TILES, m + 1)
+                    nc.vector.quantize_mx(
+                        out=a_codes_g[:, tiles, :].rearrange("p m i -> p (m i)").bitcast(FP8X4),
+                        scales=a_scales_g[:, tiles, :].rearrange("p m i -> p (m i)"),
+                        in_=a_grouped[:, tiles].rearrange("p m i t -> p (m i t)"),
+                    )
+            a_codes.append(a_codes_g)
+            a_scales.append(a_scales_g)
+
+        out_rows = out.rearrange("(b m p) c -> b p m c", m=PACK, p=P)
+        for b in range(TILES // PACK):
+            out_sum = sum_psum.tile([P, PACK, CO], F32, name="out_sum%d" % b)
+            for s in range(PACK):
+                m = PACK * b + s
+                for g in range(PASSES):
+                    nc.tensor.matmul_mx(
+                        out=out_sum[:, s, :],
+                        lhsT=a_codes[g][:, m, :].bitcast(FP8X4),
+                        lhsT_scale=a_scales[g][:, m, :],
+                        rhs=h_codes[:, g, :].bitcast(FP8X4),
+                        rhs_scale=h_scales[:, g, :],
+                        start=(g == 0),
+                        stop=(g == PASSES - 1),
+                    )
+            biased = result_pool.tile([P, PACK, CO], F32)
+            nc.vector.tensor_tensor(
+                out=biased[:],
+                in0=out_sum[:],
+                in1=bias_all[:].unsqueeze(1).to_broadcast([P, PACK, CO]),
+                op=ALU.add,
+            )
+            result = result_pool.tile([P, PACK, CO], F32)
+            nc.vector.scalar_tensor_tensor(
+                out=result[:],
+                in0=biased[:],
+                scalar=LEAKY_SLOPE,
+                in1=biased[:],
+                op0=ALU.mult,
+                op1=ALU.max,
+            )
+            nc.sync.dma_start(out=out_rows[b], in_=result[:])

@@ -19,6 +19,9 @@ CO = 128
 TILES = NODES // P
 PASSES = NODES // (P * PACK)
 QUANT_TILES = 2
+HALF = NODES // PASSES
+BANKS = 4
+H_AFTER = 6
 LEAKY_SLOPE = 0.01
 
 FLOPS = 2 * NODES * FEATS * CO + 2 * NODES * NODES * CO
@@ -27,11 +30,12 @@ FLOPS = 2 * NODES * FEATS * CO + 2 * NODES * NODES * CO
 def tile_gcnconv_s_kernel(tc, x, adj, weightr, weightd, bias, out):
     nc = tc.nc
     with ExitStack() as ctx:
+        ctx.enter_context(tc.manual_schedule())
         keep = ctx.enter_context(tc.tile_pool(name="keep", bufs=1))
         scrap_pool = ctx.enter_context(tc.tile_pool(name="scrap", bufs=2))
         result_pool = ctx.enter_context(tc.tile_pool(name="result", bufs=2))
-        flip_psum = ctx.enter_context(tc.psum_pool(name="flip", bufs=4))
-        sum_psum = ctx.enter_context(tc.psum_pool(name="sums", bufs=1))
+        flip_psum = ctx.enter_context(tc.psum_pool(name="flip", bufs=BANKS))
+        other_psum = ctx.enter_context(tc.psum_pool(name="other", bufs=4))
 
         adj_rows = adj.rearrange("(m p) j -> m p j", p=P)
         adj_sb = []
@@ -63,11 +67,27 @@ def tile_gcnconv_s_kernel(tc, x, adj, weightr, weightd, bias, out):
 
         deg = keep.tile([P, TILES], F32)
         dinv = [keep.tile([P, PACK], F32, name="dinv%d" % g) for g in range(PASSES)]
-        scaled = []
-        loop_scaled = []
-        for m in range(TILES):
-            g, t = divmod(m, PACK)
-            dinv_m = dinv[g][:, t : t + 1]
+        scaled = [
+            [keep.tile([P, HALF], F32, name="scaled%d_%d" % (m, g)) for g in range(PASSES)]
+            for m in range(TILES)
+        ]
+        loop_scaled = [keep.tile([P, P], F32, name="loop_scaled%d" % m) for m in range(TILES)]
+        flipped = {}
+        a_grouped = [
+            keep.tile([P, TILES, P, PACK], BF16, name="a_grouped%d" % g, align_bytes=64)
+            for g in range(PASSES)
+        ]
+        a_codes = [
+            keep.tile([P, TILES, P], U32, name="a_codes%d" % g, align_bytes=64) for g in range(PASSES)
+        ]
+        a_scales = [
+            keep.tile([P, TILES, P], U8, name="a_scales%d" % g, align_bytes=64) for g in range(PASSES)
+        ]
+
+        def dinv_of(m):
+            return dinv[m // PACK][:, m % PACK : m % PACK + 1]
+
+        def row_sum(m):
             scrap = scrap_pool.tile([P, NODES], BF16)
             nc.vector.tensor_scalar(
                 out=scrap[:],
@@ -78,44 +98,81 @@ def tile_gcnconv_s_kernel(tc, x, adj, weightr, weightd, bias, out):
                 op1=ALU.add,
                 accum_out=deg[:, m : m + 1],
             )
-            nc.scalar.activation(out=dinv_m, in_=deg[:, m : m + 1], func=ACT.Abs_reciprocal_sqrt)
-            scaled_m = keep.tile([P, NODES], F32, name="scaled%d" % m)
-            nc.scalar.activation(out=scaled_m[:], in_=adj_sb[m][:], func=ACT.Copy, scale=dinv_m)
-            scaled.append(scaled_m)
+
+        def self_loop(m):
             loop_m = keep.tile([P, P], F32, name="loop%d" % m)
             nc.gpsimd.tensor_tensor(
                 out=loop_m[:], in0=adj_sb[m][:, m * P : (m + 1) * P], in1=ident[:], op=ALU.add
             )
-            loop_scaled_m = keep.tile([P, P], F32, name="loop_scaled%d" % m)
             nc.gpsimd.tensor_scalar(
-                out=loop_scaled_m[:],
+                out=loop_scaled[m][:],
                 in0=loop_m[:],
-                scalar1=dinv_m,
+                scalar1=dinv_of(m),
                 scalar2=0.0,
                 op0=ALU.mult,
                 op1=ALU.add,
             )
-            loop_scaled.append(loop_scaled_m)
+
+        def scale(m, g):
+            nc.scalar.activation(
+                out=scaled[m][g][:],
+                in_=adj_sb[m][:, g * HALF : (g + 1) * HALF],
+                func=ACT.Copy,
+                scale=dinv_of(m),
+            )
+
+        def flip(m, g):
+            bank = flip_psum.tile([P, PACK, P], F32, tag="bank", name="flipped%d_%d" % (m, g))
+            for t in range(PACK):
+                if PACK * g + t == m:
+                    rows = loop_scaled[m][:]
+                else:
+                    rows = scaled[m][g][:, t * P : (t + 1) * P]
+                nc.tensor.transpose(bank[:, t, :], rows, ident[:])
+            flipped[(m, g)] = bank
+
+        def finish(m, g):
+            nc.vector.tensor_tensor(
+                out=a_grouped[g][:, m],
+                in0=flipped[(m, g)][:].rearrange("p t i -> p i t"),
+                in1=dinv[g][:].unsqueeze(1).to_broadcast([P, P, PACK]),
+                op=ALU.mult,
+            )
+
+        def quantise_a(tiles, g):
+            nc.vector.quantize_mx(
+                out=a_codes[g][:, tiles, :].rearrange("p m i -> p (m i)").bitcast(FP8X4),
+                scales=a_scales[g][:, tiles, :].rearrange("p m i -> p (m i)"),
+                in_=a_grouped[g][:, tiles].rearrange("p m i t -> p (m i t)"),
+            )
+
+        for m in range(TILES):
+            row_sum(m)
+        for m in range(TILES):
+            nc.scalar.activation(out=dinv_of(m), in_=deg[:, m : m + 1], func=ACT.Abs_reciprocal_sqrt)
+            self_loop(m)
+            scale(m, 0)
+            if m < BANKS:
+                flip(m, 0)
 
         w_grouped = keep.tile([P, 2, CO, PACK], BF16, align_bytes=64)
-        nc.scalar.copy(out=w_grouped[:], in_=w_raw[:].rearrange("p w t c -> p w c t"))
-        w_codes = keep.tile([P, 2, CO], U32, align_bytes=64)
-        w_scales = keep.tile([P, 2, CO], U8, align_bytes=64)
-        nc.vector.quantize_mx(
-            out=w_codes[:].rearrange("p w c -> p (w c)").bitcast(FP8X4),
-            scales=w_scales[:].rearrange("p w c -> p (w c)"),
-            in_=w_grouped[:].rearrange("p w c t -> p (w c t)"),
-        )
+        for w in range(2):
+            nc.gpsimd.tensor_scalar(
+                out=w_grouped[:, w],
+                in0=w_raw[:, w].rearrange("p t c -> p c t"),
+                scalar1=1.0,
+                scalar2=0.0,
+                op0=ALU.mult,
+                op1=ALU.add,
+            )
         x_grouped = keep.tile([P, NODES, PACK], BF16, align_bytes=64)
         x_words = x_grouped[:].bitcast(F32)
-        x_codes = keep.tile([P, NODES], U32, align_bytes=64)
-        x_scales = keep.tile([P, NODES], U8, align_bytes=64)
         for pair in range(TILES // 2):
-            flipped = flip_psum.tile([P, 2, 2, P], F32, tag="bank")
+            x_flipped = other_psum.tile([P, 2, 2, P], F32, tag="other")
             for n2 in range(2):
                 for u in range(2):
                     nc.tensor.transpose(
-                        flipped[:, n2, u, :],
+                        x_flipped[:, n2, u, :],
                         x_sb[:, 2 * pair + n2, :].bitcast(F32)[:, u * P : (u + 1) * P],
                         ident[:],
                     )
@@ -123,8 +180,26 @@ def tile_gcnconv_s_kernel(tc, x, adj, weightr, weightd, bias, out):
                 out=x_words[:, 2 * pair * P : (2 * pair + 2) * P, :].rearrange(
                     "p (n r) u -> p n r u", n=2
                 ),
-                in_=flipped[:].rearrange("p n u r -> p n r u"),
+                in_=x_flipped[:].rearrange("p n u r -> p n r u"),
             )
+
+        for m in range(TILES + 1):
+            if m < TILES:
+                finish(m, 0)
+            if m + BANKS < TILES:
+                flip(m + BANKS, 0)
+            if m >= QUANT_TILES and m % QUANT_TILES == 0:
+                quantise_a(slice(m - QUANT_TILES, m), 0)
+
+        w_codes = keep.tile([P, 2, CO], U32, align_bytes=64)
+        w_scales = keep.tile([P, 2, CO], U8, align_bytes=64)
+        nc.vector.quantize_mx(
+            out=w_codes[:].rearrange("p w c -> p (w c)").bitcast(FP8X4),
+            scales=w_scales[:].rearrange("p w c -> p (w c)"),
+            in_=w_grouped[:].rearrange("p w c t -> p (w c t)"),
+        )
+        x_codes = keep.tile([P, NODES], U32, align_bytes=64)
+        x_scales = keep.tile([P, NODES], U8, align_bytes=64)
         for half in range(2):
             nodes = slice(half * NODES // 2, (half + 1) * NODES // 2)
             nc.vector.quantize_mx(
@@ -132,9 +207,17 @@ def tile_gcnconv_s_kernel(tc, x, adj, weightr, weightd, bias, out):
                 scales=x_scales[:, nodes],
                 in_=x_grouped[:, nodes, :].rearrange("p r t -> p (r t)"),
             )
+
+        for m in range(TILES):
+            scale(m, 1)
+        for m in range(BANKS):
+            flip(m, 1)
+
         h_grouped = keep.tile([P, PASSES, CO, PACK], BF16, align_bytes=64)
+        h_codes = keep.tile([P, PASSES, CO], U32, align_bytes=64)
+        h_scales = keep.tile([P, PASSES, CO], U8, align_bytes=64)
         for g in range(PASSES):
-            h_sum = sum_psum.tile([P, PACK, CO], F32, name="h_sum%d" % g)
+            h_sum = other_psum.tile([P, PACK, CO], F32, tag="other")
             for t in range(PACK):
                 n = PACK * g + t
                 nc.tensor.matmul_mx(
@@ -147,64 +230,49 @@ def tile_gcnconv_s_kernel(tc, x, adj, weightr, weightd, bias, out):
                     stop=True,
                 )
             nc.scalar.copy(out=h_grouped[:, g], in_=h_sum[:].rearrange("p t c -> p c t"))
-        h_codes = keep.tile([P, PASSES, CO], U32, align_bytes=64)
-        h_scales = keep.tile([P, PASSES, CO], U8, align_bytes=64)
-        nc.vector.quantize_mx(
-            out=h_codes[:].rearrange("p g c -> p (g c)").bitcast(FP8X4),
-            scales=h_scales[:].rearrange("p g c -> p (g c)"),
-            in_=h_grouped[:].rearrange("p g c t -> p (g c t)"),
-        )
 
-        a_codes = []
-        a_scales = []
-        for g in range(PASSES):
-            a_grouped = keep.tile([P, TILES, P, PACK], BF16, name="a_grouped%d" % g, align_bytes=64)
-            a_codes_g = keep.tile([P, TILES, P], U32, name="a_codes%d" % g, align_bytes=64)
-            a_scales_g = keep.tile([P, TILES, P], U8, name="a_scales%d" % g, align_bytes=64)
-            for m in range(TILES):
-                flipped = flip_psum.tile([P, PACK, P], F32, tag="bank")
-                for t in range(PACK):
-                    block = PACK * g + t
-                    if block == m:
-                        rows = loop_scaled[m][:]
-                    else:
-                        rows = scaled[m][:, block * P : (block + 1) * P]
-                    nc.tensor.transpose(flipped[:, t, :], rows, ident[:])
-                nc.vector.tensor_tensor(
-                    out=a_grouped[:, m],
-                    in0=flipped[:].rearrange("p t i -> p i t"),
-                    in1=dinv[g][:].unsqueeze(1).to_broadcast([P, P, PACK]),
-                    op=ALU.mult,
+        out_sums = [
+            other_psum.tile([P, PACK, CO], F32, tag="other", name="out_sum%d" % b)
+            for b in range(TILES // PACK)
+        ]
+
+        def aggregate(m):
+            for g in range(PASSES):
+                nc.tensor.matmul_mx(
+                    out=out_sums[m // PACK][:, m % PACK, :],
+                    lhsT=a_codes[g][:, m, :].bitcast(FP8X4),
+                    lhsT_scale=a_scales[g][:, m, :],
+                    rhs=h_codes[:, g, :].bitcast(FP8X4),
+                    rhs_scale=h_scales[:, g, :],
+                    start=(g == 0),
+                    stop=(g == PASSES - 1),
                 )
-                if m % QUANT_TILES == QUANT_TILES - 1:
-                    tiles = slice(m + 1 - QUANT_TILES, m + 1)
+
+        for m in range(TILES + 1):
+            if m < TILES:
+                finish(m, 1)
+            if m + BANKS < TILES:
+                flip(m + BANKS, 1)
+            if m >= QUANT_TILES and m % QUANT_TILES == 0:
+                quantise_a(slice(m - QUANT_TILES, m), 1)
+                if m == H_AFTER:
                     nc.vector.quantize_mx(
-                        out=a_codes_g[:, tiles, :].rearrange("p m i -> p (m i)").bitcast(FP8X4),
-                        scales=a_scales_g[:, tiles, :].rearrange("p m i -> p (m i)"),
-                        in_=a_grouped[:, tiles].rearrange("p m i t -> p (m i t)"),
+                        out=h_codes[:].rearrange("p g c -> p (g c)").bitcast(FP8X4),
+                        scales=h_scales[:].rearrange("p g c -> p (g c)"),
+                        in_=h_grouped[:].rearrange("p g c t -> p (g c t)"),
                     )
-            a_codes.append(a_codes_g)
-            a_scales.append(a_scales_g)
+                    for row_tile in range(m - QUANT_TILES):
+                        aggregate(row_tile)
+                if m >= H_AFTER:
+                    for row_tile in range(m - QUANT_TILES, m):
+                        aggregate(row_tile)
 
         out_rows = out.rearrange("(b m p) c -> b p m c", m=PACK, p=P)
         for b in range(TILES // PACK):
-            out_sum = sum_psum.tile([P, PACK, CO], F32, name="out_sum%d" % b)
-            for s in range(PACK):
-                m = PACK * b + s
-                for g in range(PASSES):
-                    nc.tensor.matmul_mx(
-                        out=out_sum[:, s, :],
-                        lhsT=a_codes[g][:, m, :].bitcast(FP8X4),
-                        lhsT_scale=a_scales[g][:, m, :],
-                        rhs=h_codes[:, g, :].bitcast(FP8X4),
-                        rhs_scale=h_scales[:, g, :],
-                        start=(g == 0),
-                        stop=(g == PASSES - 1),
-                    )
             biased = result_pool.tile([P, PACK, CO], F32)
             nc.vector.tensor_tensor(
                 out=biased[:],
-                in0=out_sum[:],
+                in0=out_sums[b][:],
                 in1=bias_all[:].unsqueeze(1).to_broadcast([P, PACK, CO]),
                 op=ALU.add,
             )

@@ -21,7 +21,7 @@ PASSES = NODES // (P * PACK)
 QUANT_TILES = 2
 HALF = NODES // PASSES
 BANKS = 4
-H_AFTER = 6
+H_AFTER = 5
 LEAKY_SLOPE = 0.01
 
 FLOPS = 2 * NODES * FEATS * CO + 2 * NODES * NODES * CO
@@ -155,6 +155,17 @@ def tile_gcnconv_s_kernel(tc, x, adj, weightr, weightd, bias, out):
             if m < BANKS:
                 flip(m, 0)
 
+        for m in range(TILES + 1):
+            if m < TILES:
+                finish(m, 0)
+            if m + BANKS < TILES:
+                flip(m + BANKS, 0)
+            if m >= QUANT_TILES and m % QUANT_TILES == 0:
+                quantise_a(slice(m - QUANT_TILES, m), 0)
+
+        for m in range(BANKS):
+            scale(m, 1)
+
         w_grouped = keep.tile([P, 2, CO, PACK], BF16, align_bytes=64)
         for w in range(2):
             nc.gpsimd.tensor_scalar(
@@ -183,14 +194,6 @@ def tile_gcnconv_s_kernel(tc, x, adj, weightr, weightd, bias, out):
                 in_=x_flipped[:].rearrange("p n u r -> p n r u"),
             )
 
-        for m in range(TILES + 1):
-            if m < TILES:
-                finish(m, 0)
-            if m + BANKS < TILES:
-                flip(m + BANKS, 0)
-            if m >= QUANT_TILES and m % QUANT_TILES == 0:
-                quantise_a(slice(m - QUANT_TILES, m), 0)
-
         w_codes = keep.tile([P, 2, CO], U32, align_bytes=64)
         w_scales = keep.tile([P, 2, CO], U8, align_bytes=64)
         nc.vector.quantize_mx(
@@ -208,7 +211,7 @@ def tile_gcnconv_s_kernel(tc, x, adj, weightr, weightd, bias, out):
                 in_=x_grouped[:, nodes, :].rearrange("p r t -> p (r t)"),
             )
 
-        for m in range(TILES):
+        for m in range(BANKS, TILES):
             scale(m, 1)
         for m in range(BANKS):
             flip(m, 1)
@@ -248,6 +251,8 @@ def tile_gcnconv_s_kernel(tc, x, adj, weightr, weightd, bias, out):
                     stop=(g == PASSES - 1),
                 )
 
+        quantised = 0
+        aggregated = 0
         for m in range(TILES + 1):
             if m < TILES:
                 finish(m, 1)
@@ -255,17 +260,17 @@ def tile_gcnconv_s_kernel(tc, x, adj, weightr, weightd, bias, out):
                 flip(m + BANKS, 1)
             if m >= QUANT_TILES and m % QUANT_TILES == 0:
                 quantise_a(slice(m - QUANT_TILES, m), 1)
-                if m == H_AFTER:
-                    nc.vector.quantize_mx(
-                        out=h_codes[:].rearrange("p g c -> p (g c)").bitcast(FP8X4),
-                        scales=h_scales[:].rearrange("p g c -> p (g c)"),
-                        in_=h_grouped[:].rearrange("p g c t -> p (g c t)"),
-                    )
-                    for row_tile in range(m - QUANT_TILES):
-                        aggregate(row_tile)
-                if m >= H_AFTER:
-                    for row_tile in range(m - QUANT_TILES, m):
-                        aggregate(row_tile)
+                quantised = m
+            if m == H_AFTER:
+                nc.vector.quantize_mx(
+                    out=h_codes[:].rearrange("p g c -> p (g c)").bitcast(FP8X4),
+                    scales=h_scales[:].rearrange("p g c -> p (g c)"),
+                    in_=h_grouped[:].rearrange("p g c t -> p (g c t)"),
+                )
+            if m >= H_AFTER:
+                for row_tile in range(aggregated, quantised):
+                    aggregate(row_tile)
+                aggregated = quantised
 
         out_rows = out.rearrange("(b m p) c -> b p m c", m=PACK, p=P)
         for b in range(TILES // PACK):

@@ -18,11 +18,11 @@ FEATS = 512
 CO = 128
 TILES = NODES // P
 PASSES = NODES // (P * PACK)
-QUANT_TILES = 2
 HALF = NODES // PASSES
-BANKS = 4
-H_AFTER = 5
 LEAKY_SLOPE = 0.01
+SCALAR_SUMS = (1, 2, 5, 6)
+GPSIMD_TILES = (1, 5)
+LOAD_ORDER = (1, 0, 2, 3, 5, 4, 6, 7)
 
 FLOPS = 2 * NODES * FEATS * CO + 2 * NODES * NODES * CO
 
@@ -33,27 +33,30 @@ def tile_gcnconv_s_kernel(tc, x, adj, weightr, weightd, bias, out):
         ctx.enter_context(tc.manual_schedule())
         keep = ctx.enter_context(tc.tile_pool(name="keep", bufs=1))
         scrap_pool = ctx.enter_context(tc.tile_pool(name="scrap", bufs=2))
-        result_pool = ctx.enter_context(tc.tile_pool(name="result", bufs=2))
-        flip_psum = ctx.enter_context(tc.psum_pool(name="flip", bufs=BANKS))
-        other_psum = ctx.enter_context(tc.psum_pool(name="other", bufs=4))
+        result_pool = ctx.enter_context(tc.tile_pool(name="result", bufs=3))
+        spread_psum = ctx.enter_context(tc.psum_pool(name="spread", bufs=1))
+        flip_psum = ctx.enter_context(tc.psum_pool(name="flip", bufs=3))
+        other_psum = ctx.enter_context(tc.psum_pool(name="other", bufs=3))
 
         adj_rows = adj.rearrange("(m p) j -> m p j", p=P)
-        adj_sb = []
-        for m in range(TILES):
+        adj_sb = {}
+        w_raw = keep.tile([P, 2, PACK, CO], BF16)
+        for m in LOAD_ORDER:
             adj_m = keep.tile([P, NODES], BF16, name="adj%d" % m)
             nc.sync.dma_start(out=adj_m[:], in_=adj_rows[m])
-            adj_sb.append(adj_m)
-        w_raw = keep.tile([P, 2, PACK, CO], BF16)
+            adj_sb[m] = adj_m
         for w, weight in enumerate((weightr, weightd)):
             nc.sync.dma_start(
                 out=w_raw[:, w].rearrange("p (u e) c -> p u (e c)", e=2),
                 in_=weight.rearrange("(u p e) c -> p u (e c)", u=2, e=2),
             )
         x_sb = keep.tile([P, TILES, FEATS], BF16)
-        x_rows = x.rearrange("(n p) k -> p n k", p=P)
+        x_rows = x.rearrange("(v p e) k -> p v (e k)", p=P, e=2)
+        x_slots = x_sb[:].rearrange("p (v e) k -> p v (e k)", e=2)
         for half in range(2):
-            tiles = slice(half * TILES // 2, (half + 1) * TILES // 2)
-            nc.sync.dma_start(out=x_sb[:, tiles, :], in_=x_rows[:, tiles, :])
+            nc.sync.dma_start(
+                out=x_slots[:, 2 * half : 2 * half + 2], in_=x_rows[:, 2 * half : 2 * half + 2]
+            )
         bias_all = keep.tile([P, CO], BF16)
         nc.sync.dma_start(out=bias_all[:], in_=bias.partition_broadcast(P))
 
@@ -65,121 +68,173 @@ def tile_gcnconv_s_kernel(tc, x, adj, weightr, weightd, bias, out):
         warm = keep.tile([P, 1], F32)
         nc.scalar.activation(out=warm[:], in_=one[:], func=ACT.Abs_reciprocal_sqrt)
 
-        deg = keep.tile([P, TILES], F32)
+        sums = keep.tile([P, TILES], F32)
         dinv = [keep.tile([P, PACK], F32, name="dinv%d" % g) for g in range(PASSES)]
-        scaled = [
-            [keep.tile([P, HALF], F32, name="scaled%d_%d" % (m, g)) for g in range(PASSES)]
-            for m in range(TILES)
-        ]
-        loop_scaled = [keep.tile([P, P], F32, name="loop_scaled%d" % m) for m in range(TILES)]
-        flipped = {}
-        a_grouped = [
-            keep.tile([P, TILES, P, PACK], BF16, name="a_grouped%d" % g, align_bytes=64)
-            for g in range(PASSES)
-        ]
-        a_codes = [
-            keep.tile([P, TILES, P], U32, name="a_codes%d" % g, align_bytes=64) for g in range(PASSES)
-        ]
-        a_scales = [
-            keep.tile([P, TILES, P], U8, name="a_scales%d" % g, align_bytes=64) for g in range(PASSES)
-        ]
+        looped = {}
 
         def dinv_of(m):
             return dinv[m // PACK][:, m % PACK : m % PACK + 1]
 
-        def row_sum(m):
+        def diag(m):
+            return slice(m * P, (m + 1) * P)
+
+        def vector_sum(m):
             scrap = scrap_pool.tile([P, NODES], BF16)
             nc.vector.tensor_scalar(
                 out=scrap[:],
                 in0=adj_sb[m][:],
                 scalar1=1.0,
-                scalar2=1.0,
+                scalar2=0.0,
                 op0=ALU.mult,
                 op1=ALU.add,
-                accum_out=deg[:, m : m + 1],
+                accum_out=sums[:, m : m + 1],
             )
 
-        def self_loop(m):
+        def add_loop(m, engine):
             loop_m = keep.tile([P, P], F32, name="loop%d" % m)
-            nc.gpsimd.tensor_tensor(
-                out=loop_m[:], in0=adj_sb[m][:, m * P : (m + 1) * P], in1=ident[:], op=ALU.add
+            engine.tensor_tensor(
+                out=loop_m[:], in0=adj_sb[m][:, diag(m)], in1=ident[:], op=ALU.add
             )
+            looped[m] = loop_m
+
+        def scalar_sum(m):
+            full_m = keep.tile([P, NODES], F32, name="full%d" % m)
+            nc.scalar.activation(
+                out=full_m[:], in_=adj_sb[m][:], func=ACT.Copy, accum_out=sums[:, m : m + 1]
+            )
+            nc.gpsimd.tensor_tensor(
+                out=full_m[:, diag(m)], in0=full_m[:, diag(m)], in1=ident[:], op=ALU.add
+            )
+            looped[m] = full_m
+
+        spread = [
+            spread_psum.tile([P, PACK, P], F32, name="spread%d" % g) for g in range(PASSES)
+        ]
+
+        spread_sb = [keep.tile([P, HALF], F32, name="spread_sb%d" % g) for g in range(PASSES)]
+
+        def spread_out(g, bank):
+            for t in range(PACK):
+                nc.tensor.transpose(
+                    bank[:, t, :], dinv[g][:, t : t + 1].to_broadcast([P, P]), ident[:]
+                )
+
+        def invert(g):
+            nc.scalar.activation(
+                out=dinv[g][:],
+                in_=sums[:, g * PACK : (g + 1) * PACK],
+                func=ACT.Abs_reciprocal_sqrt,
+                bias=one[:],
+            )
+            spread_out(g, spread[g])
+
+        second_spread = {}
+
+        def spread_again(g):
+            bank = other_psum.tile([P, PACK, P], F32, tag="other", name="spread_copy%d" % g)
+            spread_out(g, bank)
+            second_spread[g] = bank
+
+        def copy_spread(g):
+            nc.scalar.copy(
+                out=spread_sb[g][:], in_=second_spread[g][:].rearrange("p t j -> p (t j)")
+            )
+
+        a_rows = [keep.tile([P, NODES], BF16, name="a_rows%d" % m) for m in range(TILES)]
+        a_grouped = [
+            keep.tile([P, PASSES, P, PACK], BF16, name="a_grouped%d" % m, align_bytes=64)
+            for m in range(TILES)
+        ]
+        a_codes = [
+            keep.tile([P, PASSES, P], U32, name="a_codes%d" % m, align_bytes=64)
+            for m in range(TILES)
+        ]
+        a_scales = [
+            keep.tile([P, PASSES, P], U8, name="a_scales%d" % m, align_bytes=64)
+            for m in range(TILES)
+        ]
+
+        def scale_piece(m, source, first, count):
+            g = first // HALF
+            at = first - g * HALF
+            nc.vector.scalar_tensor_tensor(
+                out=a_rows[m][:, first : first + count],
+                in0=source,
+                scalar=dinv_of(m),
+                in1=spread[g][:].rearrange("p t j -> p (t j)")[:, at : at + count],
+                op0=ALU.mult,
+                op1=ALU.mult,
+            )
+
+        def scale(m, g):
+            first = g * HALF
+            if m in SCALAR_SUMS:
+                scale_piece(m, looped[m][:, first : first + HALF], first, HALF)
+            elif m // PACK != g:
+                scale_piece(m, adj_sb[m][:, first : first + HALF], first, HALF)
+            else:
+                rest = first + P if m % PACK == 0 else first
+                scale_piece(m, looped[m][:], m * P, P)
+                scale_piece(m, adj_sb[m][:, rest : rest + HALF - P], rest, HALF - P)
+
+        row_scaled = {
+            m: keep.tile([P, NODES], F32, name="row_scaled%d" % m) for m in GPSIMD_TILES
+        }
+
+        def gpsimd_rows(m, g):
+            cols = slice(g * HALF, (g + 1) * HALF)
             nc.gpsimd.tensor_scalar(
-                out=loop_scaled[m][:],
-                in0=loop_m[:],
+                out=row_scaled[m][:, cols],
+                in0=looped[m][:, cols],
                 scalar1=dinv_of(m),
                 scalar2=0.0,
                 op0=ALU.mult,
                 op1=ALU.add,
             )
 
-        def scale(m, g):
-            nc.scalar.activation(
-                out=scaled[m][g][:],
-                in_=adj_sb[m][:, g * HALF : (g + 1) * HALF],
-                func=ACT.Copy,
-                scale=dinv_of(m),
-            )
-
-        def flip(m, g):
-            bank = flip_psum.tile([P, PACK, P], F32, tag="bank", name="flipped%d_%d" % (m, g))
-            for t in range(PACK):
-                if PACK * g + t == m:
-                    rows = loop_scaled[m][:]
-                else:
-                    rows = scaled[m][g][:, t * P : (t + 1) * P]
-                nc.tensor.transpose(bank[:, t, :], rows, ident[:])
-            flipped[(m, g)] = bank
-
-        def finish(m, g):
-            nc.vector.tensor_tensor(
-                out=a_grouped[g][:, m],
-                in0=flipped[(m, g)][:].rearrange("p t i -> p i t"),
-                in1=dinv[g][:].unsqueeze(1).to_broadcast([P, P, PACK]),
+        def gpsimd_cols(m, g):
+            cols = slice(g * HALF, (g + 1) * HALF)
+            nc.gpsimd.tensor_tensor(
+                out=a_rows[m][:, cols],
+                in0=row_scaled[m][:, cols],
+                in1=spread_sb[g][:],
                 op=ALU.mult,
             )
 
-        def quantise_a(tiles, g):
+        def flip(m, first=0, count=PASSES):
+            bank = flip_psum.tile(
+                [P, count * 2, P], F32, tag="bank", name="flipped%d_%d" % (m, first)
+            )
+            words = a_rows[m][:].bitcast(F32)
+            for w in range(count * 2):
+                at = (first * 2 + w) * P
+                nc.tensor.transpose(bank[:, w, :], words[:, at : at + P], ident[:])
+            nc.scalar.copy(
+                out=a_grouped[m][:, first : first + count]
+                .rearrange("p g i t -> p (g i t)")
+                .bitcast(F32)
+                .rearrange("p (g i u) -> p g i u", g=count, u=2),
+                in_=bank[:].rearrange("p (g u) i -> p g i u", g=count),
+            )
+
+        def quantise_a(m, first=0, count=PASSES):
+            passes = slice(first, first + count)
             nc.vector.quantize_mx(
-                out=a_codes[g][:, tiles, :].rearrange("p m i -> p (m i)").bitcast(FP8X4),
-                scales=a_scales[g][:, tiles, :].rearrange("p m i -> p (m i)"),
-                in_=a_grouped[g][:, tiles].rearrange("p m i t -> p (m i t)"),
+                out=a_codes[m][:, passes].rearrange("p g i -> p (g i)").bitcast(FP8X4),
+                scales=a_scales[m][:, passes].rearrange("p g i -> p (g i)"),
+                in_=a_grouped[m][:, passes].rearrange("p g i t -> p (g i t)"),
             )
 
-        for m in range(TILES):
-            row_sum(m)
-        for m in range(TILES):
-            nc.scalar.activation(out=dinv_of(m), in_=deg[:, m : m + 1], func=ACT.Abs_reciprocal_sqrt)
-            self_loop(m)
-            scale(m, 0)
-            if m < BANKS:
-                flip(m, 0)
-
-        for m in range(TILES + 1):
-            if m < TILES:
-                finish(m, 0)
-            if m + BANKS < TILES:
-                flip(m + BANKS, 0)
-            if m >= QUANT_TILES and m % QUANT_TILES == 0:
-                quantise_a(slice(m - QUANT_TILES, m), 0)
-
-        for m in range(BANKS):
-            scale(m, 1)
-
-        w_grouped = keep.tile([P, 2, CO, PACK], BF16, align_bytes=64)
-        for w in range(2):
-            nc.gpsimd.tensor_scalar(
-                out=w_grouped[:, w],
-                in0=w_raw[:, w].rearrange("p t c -> p c t"),
-                scalar1=1.0,
-                scalar2=0.0,
-                op0=ALU.mult,
-                op1=ALU.add,
-            )
         x_grouped = keep.tile([P, NODES, PACK], BF16, align_bytes=64)
         x_words = x_grouped[:].bitcast(F32)
-        for pair in range(TILES // 2):
-            x_flipped = other_psum.tile([P, 2, 2, P], F32, tag="other")
+        x_codes = keep.tile([P, NODES], U32, align_bytes=64)
+        x_scales = keep.tile([P, NODES], U8, align_bytes=64)
+
+        x_banks = {}
+
+        def flip_x(pair):
+            x_flipped = other_psum.tile([P, 2, 2, P], F32, tag="other", name="x_flipped%d" % pair)
+            x_banks[pair] = x_flipped
             for n2 in range(2):
                 for u in range(2):
                     nc.tensor.transpose(
@@ -187,23 +242,16 @@ def tile_gcnconv_s_kernel(tc, x, adj, weightr, weightd, bias, out):
                         x_sb[:, 2 * pair + n2, :].bitcast(F32)[:, u * P : (u + 1) * P],
                         ident[:],
                     )
+
+        def copy_x(pair):
             nc.scalar.copy(
                 out=x_words[:, 2 * pair * P : (2 * pair + 2) * P, :].rearrange(
                     "p (n r) u -> p n r u", n=2
                 ),
-                in_=x_flipped[:].rearrange("p n u r -> p n r u"),
+                in_=x_banks[pair][:].rearrange("p n u r -> p n r u"),
             )
 
-        w_codes = keep.tile([P, 2, CO], U32, align_bytes=64)
-        w_scales = keep.tile([P, 2, CO], U8, align_bytes=64)
-        nc.vector.quantize_mx(
-            out=w_codes[:].rearrange("p w c -> p (w c)").bitcast(FP8X4),
-            scales=w_scales[:].rearrange("p w c -> p (w c)"),
-            in_=w_grouped[:].rearrange("p w c t -> p (w c t)"),
-        )
-        x_codes = keep.tile([P, NODES], U32, align_bytes=64)
-        x_scales = keep.tile([P, NODES], U8, align_bytes=64)
-        for half in range(2):
+        def quantise_x(half):
             nodes = slice(half * NODES // 2, (half + 1) * NODES // 2)
             nc.vector.quantize_mx(
                 out=x_codes[:, nodes].bitcast(FP8X4),
@@ -211,15 +259,25 @@ def tile_gcnconv_s_kernel(tc, x, adj, weightr, weightd, bias, out):
                 in_=x_grouped[:, nodes, :].rearrange("p r t -> p (r t)"),
             )
 
-        for m in range(BANKS, TILES):
-            scale(m, 1)
-        for m in range(BANKS):
-            flip(m, 1)
+        w_grouped = keep.tile([P, 2, CO, PACK], BF16, align_bytes=64)
+        w_codes = keep.tile([P, 2, CO], U32, align_bytes=64)
+        w_scales = keep.tile([P, 2, CO], U8, align_bytes=64)
+
+        def group_w(w):
+            nc.scalar.copy(out=w_grouped[:, w], in_=w_raw[:, w].rearrange("p t c -> p c t"))
+
+        def quantise_w():
+            nc.vector.quantize_mx(
+                out=w_codes[:].rearrange("p w c -> p (w c)").bitcast(FP8X4),
+                scales=w_scales[:].rearrange("p w c -> p (w c)"),
+                in_=w_grouped[:].rearrange("p w c t -> p (w c t)"),
+            )
 
         h_grouped = keep.tile([P, PASSES, CO, PACK], BF16, align_bytes=64)
         h_codes = keep.tile([P, PASSES, CO], U32, align_bytes=64)
         h_scales = keep.tile([P, PASSES, CO], U8, align_bytes=64)
-        for g in range(PASSES):
+
+        def make_h(g):
             h_sum = other_psum.tile([P, PACK, CO], F32, tag="other")
             for t in range(PACK):
                 n = PACK * g + t
@@ -234,60 +292,136 @@ def tile_gcnconv_s_kernel(tc, x, adj, weightr, weightd, bias, out):
                 )
             nc.scalar.copy(out=h_grouped[:, g], in_=h_sum[:].rearrange("p t c -> p c t"))
 
-        out_sums = [
-            other_psum.tile([P, PACK, CO], F32, tag="other", name="out_sum%d" % b)
-            for b in range(TILES // PACK)
-        ]
+        def quantise_h():
+            nc.vector.quantize_mx(
+                out=h_codes[:].rearrange("p g c -> p (g c)").bitcast(FP8X4),
+                scales=h_scales[:].rearrange("p g c -> p (g c)"),
+                in_=h_grouped[:].rearrange("p g c t -> p (g c t)"),
+            )
 
-        def aggregate(m):
-            for g in range(PASSES):
+        out_rows = out.rearrange("(m p) c -> p m c", p=P)
+        out_sums = {}
+
+        def aggregate(m, passes=range(PASSES)):
+            first, count = (0, 4) if m < 4 else ((4, 3) if m < 7 else (7, 1))
+            if first not in out_sums:
+                out_sums[first] = other_psum.tile(
+                    [P, count, CO], F32, tag="other", name="out_sum%d" % first
+                )
+            for g in passes:
                 nc.tensor.matmul_mx(
-                    out=out_sums[m // PACK][:, m % PACK, :],
-                    lhsT=a_codes[g][:, m, :].bitcast(FP8X4),
-                    lhsT_scale=a_scales[g][:, m, :],
+                    out=out_sums[first][:, m - first, :],
+                    lhsT=a_codes[m][:, g, :].bitcast(FP8X4),
+                    lhsT_scale=a_scales[m][:, g, :],
                     rhs=h_codes[:, g, :].bitcast(FP8X4),
                     rhs_scale=h_scales[:, g, :],
                     start=(g == 0),
                     stop=(g == PASSES - 1),
                 )
 
-        quantised = 0
-        aggregated = 0
-        for m in range(TILES + 1):
-            if m < TILES:
-                finish(m, 1)
-            if m + BANKS < TILES:
-                flip(m + BANKS, 1)
-            if m >= QUANT_TILES and m % QUANT_TILES == 0:
-                quantise_a(slice(m - QUANT_TILES, m), 1)
-                quantised = m
-            if m == H_AFTER:
-                nc.vector.quantize_mx(
-                    out=h_codes[:].rearrange("p g c -> p (g c)").bitcast(FP8X4),
-                    scales=h_scales[:].rearrange("p g c -> p (g c)"),
-                    in_=h_grouped[:].rearrange("p g c t -> p (g c t)"),
-                )
-            if m >= H_AFTER:
-                for row_tile in range(aggregated, quantised):
-                    aggregate(row_tile)
-                aggregated = quantised
+        biased = {}
 
-        out_rows = out.rearrange("(b m p) c -> b p m c", m=PACK, p=P)
-        for b in range(TILES // PACK):
-            biased = result_pool.tile([P, PACK, CO], F32)
+        def add_bias(first, count):
+            biased_b = result_pool.tile([P, PACK, CO], F32, name="biased%d" % first)
+            biased[first] = biased_b
             nc.vector.tensor_tensor(
-                out=biased[:],
-                in0=out_sums[b][:],
-                in1=bias_all[:].unsqueeze(1).to_broadcast([P, PACK, CO]),
+                out=biased_b[:, :count],
+                in0=out_sums[first][:],
+                in1=bias_all[:].unsqueeze(1).to_broadcast([P, count, CO]),
                 op=ALU.add,
             )
+
+        def finish(first, count):
             result = result_pool.tile([P, PACK, CO], F32)
             nc.vector.scalar_tensor_tensor(
-                out=result[:],
-                in0=biased[:],
+                out=result[:, :count],
+                in0=biased[first][:, :count],
                 scalar=LEAKY_SLOPE,
-                in1=biased[:],
+                in1=biased[first][:, :count],
                 op0=ALU.mult,
                 op1=ALU.max,
             )
-            nc.sync.dma_start(out=out_rows[b], in_=result[:])
+            nc.sync.dma_start(out=out_rows[:, first : first + count], in_=result[:, :count])
+
+        scalar_sum(1)
+        vector_sum(0)
+        add_loop(0, nc.vector)
+        scalar_sum(2)
+        vector_sum(3)
+        invert(0)
+        spread_again(0)
+        add_loop(3, nc.vector)
+        scalar_sum(5)
+        vector_sum(4)
+        add_loop(4, nc.vector)
+        gpsimd_rows(1, 0)
+        gpsimd_rows(1, 1)
+        scalar_sum(6)
+        scale(0, 0)
+        vector_sum(7)
+        add_loop(7, nc.gpsimd)
+        flip_x(0)
+        invert(1)
+        spread_again(1)
+        copy_spread(0)
+        group_w(0)
+        group_w(1)
+        copy_x(0)
+        copy_spread(1)
+        gpsimd_cols(1, 0)
+        gpsimd_cols(1, 1)
+        gpsimd_rows(5, 0)
+        gpsimd_rows(5, 1)
+        gpsimd_cols(5, 0)
+        gpsimd_cols(5, 1)
+        scale(2, 0)
+        scale(3, 0)
+        flip_x(1)
+        copy_x(1)
+        scale(0, 1)
+        flip(0)
+        scale(2, 1)
+        flip_x(2)
+        copy_x(2)
+        flip_x(3)
+        copy_x(3)
+        scale(3, 1)
+        flip(2)
+        scale(4, 0)
+        quantise_w()
+        scale(4, 1)
+        quantise_x(0)
+        make_h(0)
+        flip(3)
+        scale(6, 0)
+        quantise_a(0)
+        scale(6, 1)
+        quantise_x(1)
+        make_h(1)
+        flip(1)
+        quantise_a(2)
+        flip(4)
+        scale(7, 0)
+        quantise_a(3)
+        flip(6)
+        scale(7, 1)
+        quantise_h()
+        quantise_a(1)
+        for m in (0, 2, 3, 1):
+            aggregate(m)
+        flip(5)
+        flip(7)
+        quantise_a(4)
+        aggregate(4)
+        add_bias(0, 4)
+        quantise_a(6)
+        aggregate(6)
+        finish(0, 4)
+        quantise_a(5)
+        aggregate(5)
+        quantise_a(7)
+        aggregate(7)
+        add_bias(4, 3)
+        finish(4, 3)
+        add_bias(7, 1)
+        finish(7, 1)

@@ -102,10 +102,11 @@ def tile_gcnconv_s_kernel(tc, x, adj, weightr, weightd, bias, out):
             nc.scalar.activation(
                 out=full_m[:], in_=adj_sb[m][:], func=ACT.Copy, accum_out=sums[:, m : m + 1]
             )
-            nc.gpsimd.tensor_tensor(
-                out=full_m[:, diag(m)], in0=full_m[:, diag(m)], in1=ident[:], op=ALU.add
-            )
             looped[m] = full_m
+
+        def add_loop_in_place(m):
+            block = looped[m][:, diag(m)]
+            nc.gpsimd.tensor_tensor(out=block, in0=block, in1=ident[:], op=ALU.add)
 
         spread = [
             spread_psum.tile([P, PACK, P], F32, name="spread%d" % g) for g in range(PASSES)
@@ -134,6 +135,11 @@ def tile_gcnconv_s_kernel(tc, x, adj, weightr, weightd, bias, out):
             bank = other_psum.tile([P, PACK, P], F32, tag="other", name="spread_copy%d" % g)
             spread_out(g, bank)
             second_spread[g] = bank
+
+        def vector_copy_spread(g):
+            nc.vector.tensor_copy(
+                out=spread_sb[g][:], in_=spread[g][:].rearrange("p t j -> p (t j)")
+            )
 
         def copy_spread(g):
             nc.scalar.copy(
@@ -190,6 +196,11 @@ def tile_gcnconv_s_kernel(tc, x, adj, weightr, weightd, bias, out):
                 scalar2=0.0,
                 op0=ALU.mult,
                 op1=ALU.add,
+            )
+
+        def scalar_rows(m):
+            nc.scalar.activation(
+                out=row_scaled[m][:], in_=looped[m][:], func=ACT.Copy, scale=dinv_of(m)
             )
 
         def gpsimd_cols(m, g):
@@ -345,83 +356,85 @@ def tile_gcnconv_s_kernel(tc, x, adj, weightr, weightd, bias, out):
 
         scalar_sum(1)
         vector_sum(0)
-        add_loop(0, nc.vector)
+        add_loop(0, nc.gpsimd)
+        add_loop_in_place(1)
         scalar_sum(2)
         vector_sum(3)
+        add_loop(3, nc.gpsimd)
+        add_loop_in_place(2)
         invert(0)
-        spread_again(0)
-        add_loop(3, nc.vector)
         scalar_sum(5)
         vector_sum(4)
-        add_loop(4, nc.vector)
         gpsimd_rows(1, 0)
         gpsimd_rows(1, 1)
+        add_loop(4, nc.gpsimd)
         scalar_sum(6)
-        scale(0, 0)
         vector_sum(7)
+        vector_copy_spread(0)
+        gpsimd_cols(1, 0)
         add_loop(7, nc.gpsimd)
+        add_loop_in_place(6)
+        add_loop_in_place(5)
+        scale(0, 0)
         flip_x(0)
         invert(1)
         spread_again(1)
-        copy_spread(0)
         group_w(0)
         group_w(1)
         copy_x(0)
         copy_spread(1)
-        gpsimd_cols(1, 0)
         gpsimd_cols(1, 1)
-        gpsimd_rows(5, 0)
-        gpsimd_rows(5, 1)
-        gpsimd_cols(5, 0)
-        gpsimd_cols(5, 1)
         scale(2, 0)
         scale(3, 0)
         flip_x(1)
         copy_x(1)
         scale(0, 1)
-        flip(0)
-        scale(2, 1)
         flip_x(2)
         copy_x(2)
         flip_x(3)
         copy_x(3)
+        scalar_rows(5)
+        scale(2, 1)
+        flip(0)
         scale(3, 1)
         flip(2)
         scale(4, 0)
         quantise_w()
-        scale(4, 1)
         quantise_x(0)
         make_h(0)
-        flip(3)
-        scale(6, 0)
-        quantise_a(0)
-        scale(6, 1)
         quantise_x(1)
         make_h(1)
-        flip(1)
-        quantise_a(2)
+        gpsimd_cols(5, 0)
+        gpsimd_cols(5, 1)
+        scale(4, 1)
+        flip(3)
         flip(4)
-        scale(7, 0)
-        quantise_a(3)
+        scale(6, 0)
+        scale(6, 1)
+        flip(1)
         flip(6)
+        scale(7, 0)
         scale(7, 1)
+        flip(7)
         quantise_h()
+        quantise_a(0)
+        quantise_a(2)
+        quantise_a(3)
         quantise_a(1)
         for m in (0, 2, 3, 1):
             aggregate(m)
         flip(5)
-        flip(7)
         quantise_a(4)
-        aggregate(4)
         add_bias(0, 4)
         quantise_a(6)
+        aggregate(4)
         aggregate(6)
         finish(0, 4)
-        quantise_a(5)
-        aggregate(5)
         quantise_a(7)
         aggregate(7)
-        add_bias(4, 3)
-        finish(4, 3)
+        quantise_a(5)
+        aggregate(5)
         add_bias(7, 1)
+        add_bias(4, 3)
         finish(7, 1)
+        finish(4, 3)

@@ -21,7 +21,6 @@ PASSES = NODES // (P * PACK)
 HALF = NODES // PASSES
 LEAKY_SLOPE = 0.01
 SCALAR_SUMS = (1, 2, 5, 6)
-GPSIMD_TILES = (1, 5)
 LOAD_ORDER = (1, 0, 2, 3, 5, 4, 6, 7)
 
 FLOPS = 2 * NODES * FEATS * CO + 2 * NODES * NODES * CO
@@ -111,35 +110,28 @@ def tile_gcnconv_s_kernel(tc, x, adj, weightr, weightd, bias, out):
         spread = [
             spread_psum.tile([P, PACK, P], F32, name="spread%d" % g) for g in range(PASSES)
         ]
-
         spread_sb = [keep.tile([P, HALF], F32, name="spread_sb%d" % g) for g in range(PASSES)]
 
-        def spread_out(g, bank):
-            for t in range(PACK):
+        def spread_out(first, bank, count=PACK):
+            for t in range(count):
                 nc.tensor.transpose(
-                    bank[:, t, :], dinv[g][:, t : t + 1].to_broadcast([P, P]), ident[:]
+                    bank[:, t, :], dinv_of(first + t).to_broadcast([P, P]), ident[:]
                 )
 
-        def invert(g):
+        def invert(first, tile):
             nc.scalar.activation(
-                out=dinv[g][:],
-                in_=sums[:, g * PACK : (g + 1) * PACK],
+                out=tile[:],
+                in_=sums[:, first : first + tile.shape[1]],
                 func=ACT.Abs_reciprocal_sqrt,
                 bias=one[:],
             )
-            spread_out(g, spread[g])
 
         second_spread = {}
 
         def spread_again(g):
             bank = other_psum.tile([P, PACK, P], F32, tag="other", name="spread_copy%d" % g)
-            spread_out(g, bank)
+            spread_out(PACK * g, bank)
             second_spread[g] = bank
-
-        def vector_copy_spread(g):
-            nc.vector.tensor_copy(
-                out=spread_sb[g][:], in_=spread[g][:].rearrange("p t j -> p (t j)")
-            )
 
         def copy_spread(g):
             nc.scalar.copy(
@@ -147,60 +139,63 @@ def tile_gcnconv_s_kernel(tc, x, adj, weightr, weightd, bias, out):
             )
 
         a_rows = [keep.tile([P, NODES], BF16, name="a_rows%d" % m) for m in range(TILES)]
-        a_grouped = [
-            keep.tile([P, PASSES, P, PACK], BF16, name="a_grouped%d" % m, align_bytes=64)
-            for m in range(TILES)
-        ]
-        a_codes = [
-            keep.tile([P, PASSES, P], U32, name="a_codes%d" % m, align_bytes=64)
-            for m in range(TILES)
-        ]
-        a_scales = [
-            keep.tile([P, PASSES, P], U8, name="a_scales%d" % m, align_bytes=64)
-            for m in range(TILES)
-        ]
+        a_grouped = keep.tile([P, TILES, PASSES, P, PACK], BF16, align_bytes=64)
+        a_codes = keep.tile([P, TILES, PASSES, P], U32, align_bytes=64)
+        a_scales = keep.tile([P, TILES, PASSES, P], U8, align_bytes=64)
 
-        def scale_piece(m, source, first, count):
-            g = first // HALF
-            at = first - g * HALF
+        def scale_piece(m, source, first, last, bank, base):
             nc.vector.scalar_tensor_tensor(
-                out=a_rows[m][:, first : first + count],
+                out=a_rows[m][:, first:last],
                 in0=source,
                 scalar=dinv_of(m),
-                in1=spread[g][:].rearrange("p t j -> p (t j)")[:, at : at + count],
+                in1=bank[:].rearrange("p t j -> p (t j)")[:, first - base : last - base],
                 op0=ALU.mult,
                 op1=ALU.mult,
             )
 
-        def scale(m, g):
-            first = g * HALF
+        def scale_columns(m, first, last, bank, base):
             if m in SCALAR_SUMS:
-                scale_piece(m, looped[m][:, first : first + HALF], first, HALF)
-            elif m // PACK != g:
-                scale_piece(m, adj_sb[m][:, first : first + HALF], first, HALF)
-            else:
-                rest = first + P if m % PACK == 0 else first
-                scale_piece(m, looped[m][:], m * P, P)
-                scale_piece(m, adj_sb[m][:, rest : rest + HALF - P], rest, HALF - P)
+                scale_piece(m, looped[m][:, first:last], first, last, bank, base)
+                return
+            at = m * P
+            if not first <= at < last:
+                scale_piece(m, adj_sb[m][:, first:last], first, last, bank, base)
+                return
+            if first < at:
+                scale_piece(m, adj_sb[m][:, first:at], first, at, bank, base)
+            scale_piece(m, looped[m][:], at, at + P, bank, base)
+            if at + P < last:
+                scale_piece(m, adj_sb[m][:, at + P : last], at + P, last, bank, base)
 
-        row_scaled = {
-            m: keep.tile([P, NODES], F32, name="row_scaled%d" % m) for m in GPSIMD_TILES
-        }
+        def scale(m, g):
+            scale_columns(m, g * HALF, (g + 1) * HALF, spread[g], g * HALF)
+
+        row_scaled = {}
+
+        def row_scaled_of(m):
+            if m not in row_scaled:
+                row_scaled_m = keep.tile([P, NODES], F32, name="row_scaled%d" % m)
+                row_scaled[m] = row_scaled_m
+            return row_scaled[m]
 
         def gpsimd_rows(m, g):
             cols = slice(g * HALF, (g + 1) * HALF)
             nc.gpsimd.tensor_scalar(
-                out=row_scaled[m][:, cols],
-                in0=looped[m][:, cols],
+                out=row_scaled_of(m)[:, cols],
+                in0=adj_sb[m][:, cols],
                 scalar1=dinv_of(m),
                 scalar2=0.0,
                 op0=ALU.mult,
                 op1=ALU.add,
             )
 
-        def scalar_rows(m):
+        def scalar_rows(m, g):
+            cols = slice(g * HALF, (g + 1) * HALF)
             nc.scalar.activation(
-                out=row_scaled[m][:], in_=looped[m][:], func=ACT.Copy, scale=dinv_of(m)
+                out=row_scaled_of(m)[:, cols],
+                in_=looped[m][:, cols],
+                func=ACT.Copy,
+                scale=dinv_of(m),
             )
 
         def gpsimd_cols(m, g):
@@ -212,28 +207,25 @@ def tile_gcnconv_s_kernel(tc, x, adj, weightr, weightd, bias, out):
                 op=ALU.mult,
             )
 
-        def flip(m, first=0, count=PASSES):
-            bank = flip_psum.tile(
-                [P, count * 2, P], F32, tag="bank", name="flipped%d_%d" % (m, first)
-            )
+        def flip(m):
+            bank = flip_psum.tile([P, PASSES * 2, P], F32, tag="bank", name="flipped%d" % m)
             words = a_rows[m][:].bitcast(F32)
-            for w in range(count * 2):
-                at = (first * 2 + w) * P
-                nc.tensor.transpose(bank[:, w, :], words[:, at : at + P], ident[:])
+            for w in range(PASSES * 2):
+                nc.tensor.transpose(bank[:, w, :], words[:, w * P : (w + 1) * P], ident[:])
             nc.scalar.copy(
-                out=a_grouped[m][:, first : first + count]
+                out=a_grouped[:, m]
                 .rearrange("p g i t -> p (g i t)")
                 .bitcast(F32)
-                .rearrange("p (g i u) -> p g i u", g=count, u=2),
-                in_=bank[:].rearrange("p (g u) i -> p g i u", g=count),
+                .rearrange("p (g i u) -> p g i u", g=PASSES, u=2),
+                in_=bank[:].rearrange("p (g u) i -> p g i u", g=PASSES),
             )
 
-        def quantise_a(m, first=0, count=PASSES):
-            passes = slice(first, first + count)
+        def quantise_a(first, count):
+            tiles = slice(first, first + count)
             nc.vector.quantize_mx(
-                out=a_codes[m][:, passes].rearrange("p g i -> p (g i)").bitcast(FP8X4),
-                scales=a_scales[m][:, passes].rearrange("p g i -> p (g i)"),
-                in_=a_grouped[m][:, passes].rearrange("p g i t -> p (g i t)"),
+                out=a_codes[:, tiles].rearrange("p m g i -> p (m g i)").bitcast(FP8X4),
+                scales=a_scales[:, tiles].rearrange("p m g i -> p (m g i)"),
+                in_=a_grouped[:, tiles].rearrange("p m g i t -> p (m g i t)"),
             )
 
         x_grouped = keep.tile([P, NODES, PACK], BF16, align_bytes=64)
@@ -322,8 +314,8 @@ def tile_gcnconv_s_kernel(tc, x, adj, weightr, weightd, bias, out):
             for g in passes:
                 nc.tensor.matmul_mx(
                     out=out_sums[first][:, m - first, :],
-                    lhsT=a_codes[m][:, g, :].bitcast(FP8X4),
-                    lhsT_scale=a_scales[m][:, g, :],
+                    lhsT=a_codes[:, m, g, :].bitcast(FP8X4),
+                    lhsT_scale=a_scales[:, m, g, :],
                     rhs=h_codes[:, g, :].bitcast(FP8X4),
                     rhs_scale=h_scales[:, g, :],
                     start=(g == 0),
@@ -362,79 +354,72 @@ def tile_gcnconv_s_kernel(tc, x, adj, weightr, weightd, bias, out):
         vector_sum(3)
         add_loop(3, nc.gpsimd)
         add_loop_in_place(2)
-        invert(0)
+        invert(0, dinv[0])
+        spread_out(0, spread[0])
         scalar_sum(5)
         vector_sum(4)
-        gpsimd_rows(1, 0)
         gpsimd_rows(1, 1)
+        gpsimd_rows(2, 1)
         add_loop(4, nc.gpsimd)
         scalar_sum(6)
         vector_sum(7)
-        vector_copy_spread(0)
-        gpsimd_cols(1, 0)
+        add_loop_in_place(5)
         add_loop(7, nc.gpsimd)
         add_loop_in_place(6)
-        add_loop_in_place(5)
-        scale(0, 0)
-        flip_x(0)
-        invert(1)
+        invert(4, dinv[1])
+        spread_out(4, spread[1])
         spread_again(1)
         group_w(0)
         group_w(1)
-        copy_x(0)
+        scalar_rows(5, 1)
         copy_spread(1)
+        for m in range(PACK):
+            scale(m, 0)
         gpsimd_cols(1, 1)
-        scale(2, 0)
-        scale(3, 0)
+        gpsimd_cols(2, 1)
+        gpsimd_cols(5, 1)
+        flip_x(0)
+        copy_x(0)
+        scale(0, 1)
         flip_x(1)
         copy_x(1)
-        scale(0, 1)
+        scale(3, 1)
         flip_x(2)
         copy_x(2)
         flip_x(3)
         copy_x(3)
-        scalar_rows(5)
-        scale(2, 1)
         flip(0)
-        scale(3, 1)
-        flip(2)
+        flip(3)
+        flip(1)
         scale(4, 0)
+        scale(4, 1)
+        flip(4)
+        scale(5, 0)
+        scale(6, 0)
+        flip(2)
+        scale(6, 1)
+        scale(7, 0)
+        flip(5)
+        scale(7, 1)
         quantise_w()
         quantise_x(0)
         make_h(0)
         quantise_x(1)
         make_h(1)
-        gpsimd_cols(5, 0)
-        gpsimd_cols(5, 1)
-        scale(4, 1)
-        flip(3)
-        flip(4)
-        scale(6, 0)
-        scale(6, 1)
-        flip(1)
         flip(6)
-        scale(7, 0)
-        scale(7, 1)
         flip(7)
+        quantise_a(0, 2)
+        quantise_a(2, 2)
         quantise_h()
-        quantise_a(0)
-        quantise_a(2)
-        quantise_a(3)
-        quantise_a(1)
-        for m in (0, 2, 3, 1):
+        quantise_a(4, 2)
+        for m in range(6):
             aggregate(m)
-        flip(5)
-        quantise_a(4)
-        add_bias(0, 4)
-        quantise_a(6)
-        aggregate(4)
+        quantise_a(6, 2)
         aggregate(6)
-        finish(0, 4)
-        quantise_a(7)
         aggregate(7)
-        quantise_a(5)
-        aggregate(5)
-        add_bias(7, 1)
+        add_bias(0, 4)
+        finish(0, 4)
         add_bias(4, 3)
-        finish(7, 1)
+        add_bias(7, 1)
         finish(4, 3)
+        finish(7, 1)

@@ -139,9 +139,14 @@ def tile_gcnconv_s_kernel(tc, x, adj, weightr, weightd, bias, out):
             )
 
         a_rows = [keep.tile([P, NODES], BF16, name="a_rows%d" % m) for m in range(TILES)]
-        a_grouped = keep.tile([P, TILES, PASSES, P, PACK], BF16, align_bytes=64)
-        a_codes = keep.tile([P, TILES, PASSES, P], U32, align_bytes=64)
-        a_scales = keep.tile([P, TILES, PASSES, P], U8, align_bytes=64)
+        a_grouped = keep.tile([P, TILES * PASSES, P, PACK], BF16, align_bytes=64)
+        a_codes = keep.tile([P, TILES * PASSES, P], U32, align_bytes=64)
+        a_scales = keep.tile([P, TILES * PASSES, P], U8, align_bytes=64)
+
+        def slot(m, g):
+            if m < PACK:
+                return PACK * (m // 2) + 2 * g + m % 2
+            return PASSES * m + g
 
         def scale_piece(m, source, first, last, bank, base):
             nc.vector.scalar_tensor_tensor(
@@ -207,25 +212,34 @@ def tile_gcnconv_s_kernel(tc, x, adj, weightr, weightd, bias, out):
                 op=ALU.mult,
             )
 
-        def flip(m):
-            bank = flip_psum.tile([P, PASSES * 2, P], F32, tag="bank", name="flipped%d" % m)
-            words = a_rows[m][:].bitcast(F32)
-            for w in range(PASSES * 2):
-                nc.tensor.transpose(bank[:, w, :], words[:, w * P : (w + 1) * P], ident[:])
+        def flip(*parts):
+            first = slot(*parts[0])
+            bank = flip_psum.tile([P, 2, 2, P], F32, tag="bank", name="flipped%d" % first)
+            for n, (m, g) in enumerate(parts):
+                words = a_rows[m][:].bitcast(F32)
+                for u in range(2):
+                    at = (2 * g + u) * P
+                    nc.tensor.transpose(bank[:, n, u, :], words[:, at : at + P], ident[:])
             nc.scalar.copy(
-                out=a_grouped[:, m]
-                .rearrange("p g i t -> p (g i t)")
+                out=a_grouped[:, first : first + 2]
+                .rearrange("p n i t -> p (n i t)")
                 .bitcast(F32)
-                .rearrange("p (g i u) -> p g i u", g=PASSES, u=2),
-                in_=bank[:].rearrange("p (g u) i -> p g i u", g=PASSES),
+                .rearrange("p (n i u) -> p n i u", n=2, u=2),
+                in_=bank[:].rearrange("p n u i -> p n i u"),
             )
 
+        def flip_tile(m):
+            flip((m, 0), (m, 1))
+
+        def flip_half(m, g):
+            flip((m, g), (m + 1, g))
+
         def quantise_a(first, count):
-            tiles = slice(first, first + count)
+            slots = slice(PASSES * first, PASSES * (first + count))
             nc.vector.quantize_mx(
-                out=a_codes[:, tiles].rearrange("p m g i -> p (m g i)").bitcast(FP8X4),
-                scales=a_scales[:, tiles].rearrange("p m g i -> p (m g i)"),
-                in_=a_grouped[:, tiles].rearrange("p m g i t -> p (m g i t)"),
+                out=a_codes[:, slots].rearrange("p n i -> p (n i)").bitcast(FP8X4),
+                scales=a_scales[:, slots].rearrange("p n i -> p (n i)"),
+                in_=a_grouped[:, slots].rearrange("p n i t -> p (n i t)"),
             )
 
         x_grouped = keep.tile([P, NODES, PACK], BF16, align_bytes=64)
@@ -314,8 +328,8 @@ def tile_gcnconv_s_kernel(tc, x, adj, weightr, weightd, bias, out):
             for g in passes:
                 nc.tensor.matmul_mx(
                     out=out_sums[first][:, m - first, :],
-                    lhsT=a_codes[:, m, g, :].bitcast(FP8X4),
-                    lhsT_scale=a_scales[:, m, g, :],
+                    lhsT=a_codes[:, slot(m, g), :].bitcast(FP8X4),
+                    lhsT_scale=a_scales[:, slot(m, g), :],
                     rhs=h_codes[:, g, :].bitcast(FP8X4),
                     rhs_scale=h_scales[:, g, :],
                     start=(g == 0),
@@ -348,18 +362,19 @@ def tile_gcnconv_s_kernel(tc, x, adj, weightr, weightd, bias, out):
 
         scalar_sum(1)
         vector_sum(0)
-        add_loop(0, nc.gpsimd)
+        add_loop(0, nc.vector)
         add_loop_in_place(1)
         scalar_sum(2)
         vector_sum(3)
-        add_loop(3, nc.gpsimd)
+        add_loop(3, nc.vector)
         add_loop_in_place(2)
         invert(0, dinv[0])
         spread_out(0, spread[0])
+        spread_again(0)
+
         scalar_sum(5)
         vector_sum(4)
-        gpsimd_rows(1, 1)
-        gpsimd_rows(2, 1)
+
         add_loop(4, nc.gpsimd)
         scalar_sum(6)
         vector_sum(7)
@@ -368,58 +383,66 @@ def tile_gcnconv_s_kernel(tc, x, adj, weightr, weightd, bias, out):
         add_loop_in_place(6)
         invert(4, dinv[1])
         spread_out(4, spread[1])
-        spread_again(1)
+        copy_spread(0)
+
+        gpsimd_rows(5, 0)
+        gpsimd_rows(6, 0)
+        gpsimd_cols(5, 0)
+        gpsimd_cols(6, 0)
+
         group_w(0)
         group_w(1)
-        scalar_rows(5, 1)
-        copy_spread(1)
-        for m in range(PACK):
-            scale(m, 0)
-        gpsimd_cols(1, 1)
-        gpsimd_cols(2, 1)
-        gpsimd_cols(5, 1)
+        scale(0, 0)
+        scale(1, 0)
+        flip_half(0, 0)
+        scale(2, 0)
+        scale(3, 0)
         flip_x(0)
         copy_x(0)
-        scale(0, 1)
+        flip_half(2, 0)
         flip_x(1)
         copy_x(1)
-        scale(3, 1)
+        scale(0, 1)
+        scale(1, 1)
         flip_x(2)
         copy_x(2)
         flip_x(3)
         copy_x(3)
-        flip(0)
-        flip(3)
-        flip(1)
+        flip_half(0, 1)
+        scale(2, 1)
+        scale(3, 1)
+        flip_half(2, 1)
         scale(4, 0)
-        scale(4, 1)
-        flip(4)
-        scale(5, 0)
-        scale(6, 0)
-        flip(2)
-        scale(6, 1)
-        scale(7, 0)
-        flip(5)
-        scale(7, 1)
         quantise_w()
         quantise_x(0)
-        make_h(0)
+        scale(4, 1)
         quantise_x(1)
+
+        make_h(0)
         make_h(1)
-        flip(6)
-        flip(7)
+        flip_tile(4)
+        scale(5, 1)
+        flip_tile(5)
         quantise_a(0, 2)
-        quantise_a(2, 2)
+        scale(6, 1)
+        flip_tile(6)
         quantise_h()
-        quantise_a(4, 2)
-        for m in range(6):
+        quantise_a(2, 2)
+        for m in range(4):
             aggregate(m)
-        quantise_a(6, 2)
-        aggregate(6)
-        aggregate(7)
+        scale(7, 0)
+        scale(7, 1)
+        flip_tile(7)
+        quantise_a(4, 2)
+        aggregate(4)
+        aggregate(5)
         add_bias(0, 4)
+        quantise_a(6, 1)
+        aggregate(6)
         finish(0, 4)
+        quantise_a(7, 1)
+        aggregate(7)
         add_bias(4, 3)
-        add_bias(7, 1)
         finish(4, 3)
+        add_bias(7, 1)
         finish(7, 1)

@@ -44,11 +44,6 @@ def tile_gcnconv_s_kernel(tc, x, adj, weightr, weightd, bias, out):
             adj_m = keep.tile([P, NODES], BF16, name="adj%d" % m)
             nc.sync.dma_start(out=adj_m[:], in_=adj_rows[m])
             adj_sb[m] = adj_m
-        for w, weight in enumerate((weightr, weightd)):
-            nc.sync.dma_start(
-                out=w_raw[:, w].rearrange("p (u e) c -> p u (e c)", e=2),
-                in_=weight.rearrange("(u p e) c -> p u (e c)", u=2, e=2),
-            )
         x_sb = keep.tile([P, TILES, FEATS], BF16)
         x_rows = x.rearrange("(v p e) k -> p v (e k)", p=P, e=2)
         x_slots = x_sb[:].rearrange("p (v e) k -> p v (e k)", e=2)
@@ -56,6 +51,12 @@ def tile_gcnconv_s_kernel(tc, x, adj, weightr, weightd, bias, out):
             nc.sync.dma_start(
                 out=x_slots[:, 2 * half : 2 * half + 2], in_=x_rows[:, 2 * half : 2 * half + 2]
             )
+            if half == 0:
+                for w, weight in enumerate((weightr, weightd)):
+                    nc.sync.dma_start(
+                        out=w_raw[:, w].rearrange("p (u e) c -> p u (e c)", e=2),
+                        in_=weight.rearrange("(u p e) c -> p u (e c)", u=2, e=2),
+                    )
         bias_all = keep.tile([P, CO], BF16)
         nc.sync.dma_start(out=bias_all[:], in_=bias.partition_broadcast(P))
 
@@ -198,7 +199,7 @@ def tile_gcnconv_s_kernel(tc, x, adj, weightr, weightd, bias, out):
             cols = slice(g * HALF, (g + 1) * HALF)
             nc.scalar.activation(
                 out=row_scaled_of(m)[:, cols],
-                in_=looped[m][:, cols],
+                in_=adj_sb[m][:, cols],
                 func=ACT.Copy,
                 scale=dinv_of(m),
             )
@@ -371,25 +372,23 @@ def tile_gcnconv_s_kernel(tc, x, adj, weightr, weightd, bias, out):
         invert(0, dinv[0])
         spread_out(0, spread[0])
         spread_again(0)
-
         scalar_sum(5)
         vector_sum(4)
-
-        add_loop(4, nc.gpsimd)
+        add_loop(4, nc.vector)
         scalar_sum(6)
         vector_sum(7)
-        add_loop_in_place(5)
         add_loop(7, nc.gpsimd)
+        add_loop_in_place(5)
         add_loop_in_place(6)
+        flip_x(0)
         invert(4, dinv[1])
         spread_out(4, spread[1])
         copy_spread(0)
-
         gpsimd_rows(5, 0)
         gpsimd_rows(6, 0)
         gpsimd_cols(5, 0)
         gpsimd_cols(6, 0)
-
+        copy_x(0)
         group_w(0)
         group_w(1)
         scale(0, 0)
@@ -397,8 +396,6 @@ def tile_gcnconv_s_kernel(tc, x, adj, weightr, weightd, bias, out):
         flip_half(0, 0)
         scale(2, 0)
         scale(3, 0)
-        flip_x(0)
-        copy_x(0)
         flip_half(2, 0)
         flip_x(1)
         copy_x(1)
@@ -413,11 +410,10 @@ def tile_gcnconv_s_kernel(tc, x, adj, weightr, weightd, bias, out):
         scale(3, 1)
         flip_half(2, 1)
         scale(4, 0)
+        scale(4, 1)
         quantise_w()
         quantise_x(0)
-        scale(4, 1)
         quantise_x(1)
-
         make_h(0)
         make_h(1)
         flip_tile(4)
@@ -426,8 +422,8 @@ def tile_gcnconv_s_kernel(tc, x, adj, weightr, weightd, bias, out):
         quantise_a(0, 2)
         scale(6, 1)
         flip_tile(6)
-        quantise_h()
         quantise_a(2, 2)
+        quantise_h()
         for m in range(4):
             aggregate(m)
         scale(7, 0)

@@ -152,9 +152,9 @@ def tile_gcnconv_s_kernel(tc, x, adj, weightr, weightd, bias, out):
         def scale_piece(m, source, first, last, bank, base):
             nc.vector.scalar_tensor_tensor(
                 out=a_rows[m][:, first:last],
-                in0=source,
+                in0=bank[:].rearrange("p t j -> p (t j)")[:, first - base : last - base],
                 scalar=dinv_of(m),
-                in1=bank[:].rearrange("p t j -> p (t j)")[:, first - base : last - base],
+                in1=source,
                 op0=ALU.mult,
                 op1=ALU.mult,
             )

from contextlib import ExitStack

import concourse.mybir as mybir
from concourse.masks import make_identity

FP8X4 = mybir.dt.float8_e4m3fn_x4
BF16 = mybir.dt.bfloat16
F32 = mybir.dt.float32
U32 = mybir.dt.uint32
U8 = mybir.dt.uint8
ALU = mybir.AluOpType
ACT = mybir.ActivationFunctionType

P = 128
PACK = 4
NODES = 1024
FEATS = 512
CO = 128
TILES = NODES // P
PASSES = NODES // (P * PACK)
HALF = NODES // PASSES
LEAKY_SLOPE = 0.01
SCALAR_SUMS = (1, 2, 5, 6)
LOAD_ORDER = (1, 0, 2, 3, 5, 4, 6, 7)

FLOPS = 2 * NODES * FEATS * CO + 2 * NODES * NODES * CO


def tile_gcnconv_s_kernel(tc, x, adj, weightr, weightd, bias, out):
    nc = tc.nc
    with ExitStack() as ctx:
        ctx.enter_context(tc.manual_schedule())
        keep = ctx.enter_context(tc.tile_pool(name="keep", bufs=1))
        scrap_pool = ctx.enter_context(tc.tile_pool(name="scrap", bufs=2))
        result_pool = ctx.enter_context(tc.tile_pool(name="result", bufs=3))
        spread_psum = ctx.enter_context(tc.psum_pool(name="spread", bufs=1))
        flip_psum = ctx.enter_context(tc.psum_pool(name="flip", bufs=3))
        other_psum = ctx.enter_context(tc.psum_pool(name="other", bufs=3))

        adj_rows = adj.rearrange("(m p) j -> m p j", p=P)
        adj_sb = {}
        w_raw = keep.tile([P, 2, PACK, CO], BF16)
        for m in LOAD_ORDER:
            adj_m = keep.tile([P, NODES], BF16, name="adj%d" % m)
            nc.sync.dma_start(out=adj_m[:], in_=adj_rows[m])
            adj_sb[m] = adj_m
        x_sb = keep.tile([P, TILES, FEATS], BF16)
        x_rows = x.rearrange("(v p e) k -> p v (e k)", p=P, e=2)
        x_slots = x_sb[:].rearrange("p (v e) k -> p v (e k)", e=2)
        for half in range(2):
            nc.sync.dma_start(
                out=x_slots[:, 2 * half : 2 * half + 2], in_=x_rows[:, 2 * half : 2 * half + 2]
            )
            if half == 0:
                for w, weight in enumerate((weightr, weightd)):
                    nc.sync.dma_start(
                        out=w_raw[:, w].rearrange("p (u e) c -> p u (e c)", e=2),
                        in_=weight.rearrange("(u p e) c -> p u (e c)", u=2, e=2),
                    )
        bias_all = keep.tile([P, CO], BF16)
        nc.sync.dma_start(out=bias_all[:], in_=bias.partition_broadcast(P))

        ident = keep.tile([P, P], F32)
        make_identity(nc, ident[:])

        one = keep.tile([P, 1], F32)
        nc.vector.memset(one[:], 1.0)
        warm = keep.tile([P, 1], F32)
        nc.scalar.activation(out=warm[:], in_=one[:], func=ACT.Abs_reciprocal_sqrt)

        sums = keep.tile([P, TILES], F32)
        dinv = [keep.tile([P, PACK], F32, name="dinv%d" % g) for g in range(PASSES)]
        looped = {}

        def dinv_of(m):
            return dinv[m // PACK][:, m % PACK : m % PACK + 1]

        def diag(m):
            return slice(m * P, (m + 1) * P)

        def vector_sum(m):
            scrap = scrap_pool.tile([P, NODES], BF16)
            nc.vector.tensor_scalar(
                out=scrap[:],
                in0=adj_sb[m][:],
                scalar1=1.0,
                scalar2=0.0,
                op0=ALU.mult,
                op1=ALU.add,
                accum_out=sums[:, m : m + 1],
            )

        def add_loop(m, engine):
            loop_m = keep.tile([P, P], F32, name="loop%d" % m)
            engine.tensor_tensor(
                out=loop_m[:], in0=adj_sb[m][:, diag(m)], in1=ident[:], op=ALU.add
            )
            looped[m] = loop_m

        def scalar_sum(m):
            full_m = keep.tile([P, NODES], F32, name="full%d" % m)
            nc.scalar.activation(
                out=full_m[:], in_=adj_sb[m][:], func=ACT.Copy, accum_out=sums[:, m : m + 1]
            )
            looped[m] = full_m

        def add_loop_in_place(m):
            block = looped[m][:, diag(m)]
            nc.gpsimd.tensor_tensor(out=block, in0=block, in1=ident[:], op=ALU.add)

        spread = [
            spread_psum.tile([P, PACK, P], F32, name="spread%d" % g) for g in range(PASSES)
        ]
        spread_sb = [keep.tile([P, HALF], F32, name="spread_sb%d" % g) for g in range(PASSES)]

        def spread_out(first, bank, count=PACK):
            for t in range(count):
                nc.tensor.transpose(
                    bank[:, t, :], dinv_of(first + t).to_broadcast([P, P]), ident[:]
                )

        def invert(first, tile):
            nc.scalar.activation(
                out=tile[:],
                in_=sums[:, first : first + tile.shape[1]],
                func=ACT.Abs_reciprocal_sqrt,
                bias=one[:],
            )

        second_spread = {}

        def spread_again(g):
            bank = other_psum.tile([P, PACK, P], F32, tag="other", name="spread_copy%d" % g)
            spread_out(PACK * g, bank)
            second_spread[g] = bank

        def copy_spread(g):
            nc.scalar.copy(
                out=spread_sb[g][:], in_=second_spread[g][:].rearrange("p t j -> p (t j)")
            )

        a_rows = [keep.tile([P, NODES], BF16, name="a_rows%d" % m) for m in range(TILES)]
        a_grouped = keep.tile([P, TILES * PASSES, P, PACK], BF16, align_bytes=64)
        a_codes = keep.tile([P, TILES * PASSES, P], U32, align_bytes=64)
        a_scales = keep.tile([P, TILES * PASSES, P], U8, align_bytes=64)

        def slot(m, g):
            if m < PACK:
                return PACK * (m // 2) + 2 * g + m % 2
            return PASSES * m + g

        def scale_piece(m, source, first, last, bank, base):
            nc.vector.scalar_tensor_tensor(
                out=a_rows[m][:, first:last],
                in0=bank[:].rearrange("p t j -> p (t j)")[:, first - base : last - base],
                scalar=dinv_of(m),
                in1=source,
                op0=ALU.mult,
                op1=ALU.mult,
            )

        def scale_columns(m, first, last, bank, base):
            if m in SCALAR_SUMS:
                scale_piece(m, looped[m][:, first:last], first, last, bank, base)
                return
            at = m * P
            if not first <= at < last:
                scale_piece(m, adj_sb[m][:, first:last], first, last, bank, base)
                return
            if first < at:
                scale_piece(m, adj_sb[m][:, first:at], first, at, bank, base)
            scale_piece(m, looped[m][:], at, at + P, bank, base)
            if at + P < last:
                scale_piece(m, adj_sb[m][:, at + P : last], at + P, last, bank, base)

        def scale(m, g):
            scale_columns(m, g * HALF, (g + 1) * HALF, spread[g], g * HALF)

        row_scaled = {}

        def row_scaled_of(m):
            if m not in row_scaled:
                row_scaled_m = keep.tile([P, NODES], F32, name="row_scaled%d" % m)
                row_scaled[m] = row_scaled_m
            return row_scaled[m]

        def gpsimd_rows(m, g):
            cols = slice(g * HALF, (g + 1) * HALF)
            nc.gpsimd.tensor_scalar(
                out=row_scaled_of(m)[:, cols],
                in0=adj_sb[m][:, cols],
                scalar1=dinv_of(m),
                scalar2=0.0,
                op0=ALU.mult,
                op1=ALU.add,
            )

        def scalar_rows(m, g):
            cols = slice(g * HALF, (g + 1) * HALF)
            nc.scalar.activation(
                out=row_scaled_of(m)[:, cols],
                in_=adj_sb[m][:, cols],
                func=ACT.Copy,
                scale=dinv_of(m),
            )

        def gpsimd_cols(m, g):
            cols = slice(g * HALF, (g + 1) * HALF)
            nc.gpsimd.tensor_tensor(
                out=a_rows[m][:, cols],
                in0=row_scaled[m][:, cols],
                in1=spread_sb[g][:],
                op=ALU.mult,
            )

        def flip(*parts):
            first = slot(*parts[0])
            bank = flip_psum.tile([P, 2, 2, P], F32, tag="bank", name="flipped%d" % first)
            for n, (m, g) in enumerate(parts):
                words = a_rows[m][:].bitcast(F32)
                for u in range(2):
                    at = (2 * g + u) * P
                    nc.tensor.transpose(bank[:, n, u, :], words[:, at : at + P], ident[:])
            nc.scalar.copy(
                out=a_grouped[:, first : first + 2]
                .rearrange("p n i t -> p (n i t)")
                .bitcast(F32)
                .rearrange("p (n i u) -> p n i u", n=2, u=2),
                in_=bank[:].rearrange("p n u i -> p n i u"),
            )

        def flip_tile(m):
            flip((m, 0), (m, 1))

        def flip_half(m, g):
            flip((m, g), (m + 1, g))

        def quantise_a(first, count):
            slots = slice(PASSES * first, PASSES * (first + count))
            nc.vector.quantize_mx(
                out=a_codes[:, slots].rearrange("p n i -> p (n i)").bitcast(FP8X4),
                scales=a_scales[:, slots].rearrange("p n i -> p (n i)"),
                in_=a_grouped[:, slots].rearrange("p n i t -> p (n i t)"),
            )

        x_grouped = keep.tile([P, NODES, PACK], BF16, align_bytes=64)
        x_words = x_grouped[:].bitcast(F32)
        x_codes = keep.tile([P, NODES], U32, align_bytes=64)
        x_scales = keep.tile([P, NODES], U8, align_bytes=64)

        x_banks = {}

        def flip_x(pair):
            x_flipped = other_psum.tile([P, 2, 2, P], F32, tag="other", name="x_flipped%d" % pair)
            x_banks[pair] = x_flipped
            for n2 in range(2):
                for u in range(2):
                    nc.tensor.transpose(
                        x_flipped[:, n2, u, :],
                        x_sb[:, 2 * pair + n2, :].bitcast(F32)[:, u * P : (u + 1) * P],
                        ident[:],
                    )

        def copy_x(pair):
            nc.scalar.copy(
                out=x_words[:, 2 * pair * P : (2 * pair + 2) * P, :].rearrange(
                    "p (n r) u -> p n r u", n=2
                ),
                in_=x_banks[pair][:].rearrange("p n u r -> p n r u"),
            )

        def quantise_x(half):
            nodes = slice(half * NODES // 2, (half + 1) * NODES // 2)
            nc.vector.quantize_mx(
                out=x_codes[:, nodes].bitcast(FP8X4),
                scales=x_scales[:, nodes],
                in_=x_grouped[:, nodes, :].rearrange("p r t -> p (r t)"),
            )

        w_grouped = keep.tile([P, 2, CO, PACK], BF16, align_bytes=64)
        w_codes = keep.tile([P, 2, CO], U32, align_bytes=64)
        w_scales = keep.tile([P, 2, CO], U8, align_bytes=64)

        def group_w(w):
            nc.scalar.copy(out=w_grouped[:, w], in_=w_raw[:, w].rearrange("p t c -> p c t"))

        def quantise_w():
            nc.vector.quantize_mx(
                out=w_codes[:].rearrange("p w c -> p (w c)").bitcast(FP8X4),
                scales=w_scales[:].rearrange("p w c -> p (w c)"),
                in_=w_grouped[:].rearrange("p w c t -> p (w c t)"),
            )

        h_grouped = keep.tile([P, PASSES, CO, PACK], BF16, align_bytes=64)
        h_codes = keep.tile([P, PASSES, CO], U32, align_bytes=64)
        h_scales = keep.tile([P, PASSES, CO], U8, align_bytes=64)

        def make_h(g):
            h_sum = other_psum.tile([P, PACK, CO], F32, tag="other")
            for t in range(PACK):
                n = PACK * g + t
                nc.tensor.matmul_mx(
                    out=h_sum[:, t, :],
                    lhsT=x_codes[:, n * P : (n + 1) * P].bitcast(FP8X4),
                    lhsT_scale=x_scales[:, n * P : (n + 1) * P],
                    rhs=w_codes[:, g, :].bitcast(FP8X4),
                    rhs_scale=w_scales[:, g, :],
                    start=True,
                    stop=True,
                )
            nc.scalar.copy(out=h_grouped[:, g], in_=h_sum[:].rearrange("p t c -> p c t"))

        def quantise_h():
            nc.vector.quantize_mx(
                out=h_codes[:].rearrange("p g c -> p (g c)").bitcast(FP8X4),
                scales=h_scales[:].rearrange("p g c -> p (g c)"),
                in_=h_grouped[:].rearrange("p g c t -> p (g c t)"),
            )

        out_rows = out.rearrange("(m p) c -> p m c", p=P)
        out_sums = {}

        def aggregate(m, passes=range(PASSES)):
            first, count = (0, 4) if m < 4 else ((4, 3) if m < 7 else (7, 1))
            if first not in out_sums:
                out_sums[first] = other_psum.tile(
                    [P, count, CO], F32, tag="other", name="out_sum%d" % first
                )
            for g in passes:
                nc.tensor.matmul_mx(
                    out=out_sums[first][:, m - first, :],
                    lhsT=a_codes[:, slot(m, g), :].bitcast(FP8X4),
                    lhsT_scale=a_scales[:, slot(m, g), :],
                    rhs=h_codes[:, g, :].bitcast(FP8X4),
                    rhs_scale=h_scales[:, g, :],
                    start=(g == 0),
                    stop=(g == PASSES - 1),
                )

        biased = {}

        def add_bias(first, count):
            biased_b = result_pool.tile([P, PACK, CO], F32, name="biased%d" % first)
            biased[first] = biased_b
            nc.vector.tensor_tensor(
                out=biased_b[:, :count],
                in0=out_sums[first][:],
                in1=bias_all[:].unsqueeze(1).to_broadcast([P, count, CO]),
                op=ALU.add,
            )

        def finish(first, count):
            result = result_pool.tile([P, PACK, CO], F32)
            nc.vector.scalar_tensor_tensor(
                out=result[:, :count],
                in0=biased[first][:, :count],
                scalar=LEAKY_SLOPE,
                in1=biased[first][:, :count],
                op0=ALU.mult,
                op1=ALU.max,
            )
            nc.sync.dma_start(out=out_rows[:, first : first + count], in_=result[:, :count])

        scalar_sum(1)
        vector_sum(0)
        add_loop(0, nc.vector)
        add_loop_in_place(1)
        scalar_sum(2)
        vector_sum(3)
        add_loop(3, nc.vector)
        add_loop_in_place(2)
        invert(0, dinv[0])
        spread_out(0, spread[0])
        spread_again(0)
        scalar_sum(5)
        vector_sum(4)
        add_loop(4, nc.vector)
        scalar_sum(6)
        vector_sum(7)
        add_loop(7, nc.gpsimd)
        add_loop_in_place(5)
        add_loop_in_place(6)
        flip_x(0)
        invert(4, dinv[1])
        spread_out(4, spread[1])
        copy_spread(0)
        gpsimd_rows(5, 0)
        gpsimd_rows(6, 0)
        gpsimd_cols(5, 0)
        gpsimd_cols(6, 0)
        copy_x(0)
        group_w(0)
        group_w(1)
        scale(0, 0)
        scale(1, 0)
        flip_half(0, 0)
        scale(2, 0)
        scale(3, 0)
        flip_half(2, 0)
        flip_x(1)
        copy_x(1)
        scale(0, 1)
        scale(1, 1)
        flip_x(2)
        copy_x(2)
        flip_x(3)
        copy_x(3)
        flip_half(0, 1)
        scale(2, 1)
        scale(3, 1)
        flip_half(2, 1)
        scale(4, 0)
        scale(4, 1)
        quantise_w()
        quantise_x(0)
        quantise_x(1)
        make_h(0)
        make_h(1)
        flip_tile(4)
        scale(5, 1)
        flip_tile(5)
        quantise_a(0, 2)
        scale(6, 1)
        flip_tile(6)
        quantise_a(2, 2)
        quantise_h()
        for m in range(4):
            aggregate(m)
        scale(7, 0)
        scale(7, 1)
        flip_tile(7)
        quantise_a(4, 2)
        aggregate(4)
        aggregate(5)
        add_bias(0, 4)
        quantise_a(6, 1)
        aggregate(6)
        finish(0, 4)
        quantise_a(7, 1)
        aggregate(7)
        add_bias(4, 3)
        finish(4, 3)
        add_bias(7, 1)
        finish(7, 1)
